import numpy as np
import ml_dtypes

BF16 = ml_dtypes.bfloat16


def bf(x):
    return np.asarray(x, np.float32).astype(BF16)


def f32(x):
    return np.asarray(x, np.float32)


def f64(x):
    return np.asarray(x).astype(np.float64)


def striped(idx):
    return np.tile(idx.reshape(-1, 16).T, (8, 1))


S, D, Q, M, B, A, K, N = 512, 128, 128, 512, 4, 64, 3, 256
WIDTH = 0.5
R_MAX = 10.0
ERF_LIM = 6.0
ERF_TERMS = 150


def erf(a):
    c = np.clip(a, -ERF_LIM, ERF_LIM)
    term = c.copy()
    total = c.copy()
    for n in range(1, ERF_TERMS):
        term = term * (2.0 * c * c) / (2.0 * n + 1.0)
        total = total + term
    r = 2.0 / np.sqrt(np.pi) * np.exp(-c * c) * total
    return np.where(np.abs(a) > ERF_LIM, np.sign(a), r)


def setup_inputs():
    return {"table": bf(np.random.standard_normal((S, D))), "w_emb": bf(np.random.standard_normal((D, M)) / np.sqrt(D + Q)), "coords": f32(3.0 * np.random.standard_normal((K, N))), "centers": f32(np.linspace(0.0, R_MAX, Q)[:, None]), "w_rbf": bf(np.random.standard_normal((Q, M)) / np.sqrt(D + Q)), "b1": f32(0.1 * np.random.standard_normal((M, 1))), "w2": bf(np.random.standard_normal((M, M)) / np.sqrt(M)), "b2": f32(0.1 * np.random.standard_normal((M, 1))), "offs": striped(np.random.permutation(np.tile(np.arange(S), 2))[:N])}


def reference(table, w_emb, coords, centers, w_rbf, b1, w2, b2, offs):
    idx = offs[:16].T.reshape(-1)
    c = f64(coords).reshape(K, B, A)
    diff = c[:, :, :, None] - c[:, :, None, :]
    dist = np.sqrt((diff * diff).sum(axis=0))
    gauss = np.exp(-0.5 * np.square((dist[None] - f64(centers)[:, :, None, None]) / WIDTH))
    rbf = gauss.mean(axis=-1).reshape(Q, N)
    pre = f64(w_emb).T @ f64(table)[idx].T + f64(w_rbf).T @ rbf + f64(b1)
    hid = 0.5 * pre * (1.0 + erf(pre / np.sqrt(2.0)))
    return f64(w2).T @ hid + f64(b2)

@@ -1,0 +1,121 @@
+import concourse.mybir as mybir
+from concourse.masks import make_identity
+
+F32 = mybir.dt.float32
+BF16 = mybir.dt.bfloat16
+U16 = mybir.dt.uint16
+ALU = mybir.AluOpType
+ACT = mybir.ActivationFunctionType
+AX = mybir.AxisListType
+
+P = 128
+S = 512
+M = 512
+N = 256
+A = 64
+Q = 128
+MB = M // P
+NB = N // P
+QC = 32
+
+FLOPS = 2 * N * (P * M + Q * M + M * M)
+
+
+def tile_frozenmlipencoder_kernel(tc, table, w_emb, coords, centers, w_rbf, b1, w2, b2, offs, out):
+    nc = tc.nc
+    with (
+        tc.tile_pool(name="held", bufs=1) as held,
+        tc.tile_pool(name="work", bufs=3) as work,
+        tc.psum_pool(name="flip", bufs=1) as flip,
+        tc.psum_pool(name="acc", bufs=4) as acc,
+    ):
+        offsets = held.tile([P, N // 16], U16, name="offsets")
+        nc.sync.dma_start(offsets[:], offs)
+
+        near = held.tile([P, NB, 3, A], F32, name="near")
+        for mol in range(N // A):
+            half, b = mol % 2, mol // 2
+            nc.sync.dma_start(
+                near[half * A : (half + 1) * A, b, :, :],
+                coords[:, mol * A : (mol + 1) * A].unsqueeze(0).to_broadcast([A, 3, A]),
+            )
+        own = held.tile([P, NB, 8], F32, name="own")
+        b1_sb = held.tile([P, MB], F32, name="b1_sb")
+        b2_sb = held.tile([P, MB], F32, name="b2_sb")
+        with nc.allow_non_contiguous_dma(reason="one float to a partition: small vectors"):
+            for b in range(NB):
+                nc.sync.dma_start(own[:, b, 0:3], coords[:, b * P : (b + 1) * P].rearrange("a p -> p a"))
+            nc.sync.dma_start(b1_sb[:], b1.rearrange("(k p) o -> p (k o)", p=P))
+            nc.sync.dma_start(b2_sb[:], b2.rearrange("(k p) o -> p (k o)", p=P))
+        centre_row = held.tile([P, Q], F32, name="centre_row")
+        nc.sync.dma_start(centre_row[:], centers.rearrange("q o -> o q").to_broadcast([P, Q]))
+
+        table_rows = held.tile([P, S // P, P], BF16, name="table_rows")
+        nc.scalar.dma_start(table_rows[:], table.rearrange("(k p) d -> p k d", p=P))
+        w_emb_sb = held.tile([P, M], BF16, name="w_emb_sb")
+        nc.scalar.dma_start(w_emb_sb[:], w_emb)
+        w_rbf_sb = held.tile([P, M], BF16, name="w_rbf_sb")
+        nc.scalar.dma_start(w_rbf_sb[:], w_rbf)
+        w2_sb = held.tile([P, MB, M], BF16, name="w2_sb")
+        nc.scalar.dma_start(w2_sb[:], w2.rearrange("(k p) n -> p k n", p=P))
+
+        ident_f = held.tile([P, P], F32, name="ident_f")
+        make_identity(nc, ident_f[:])
+        ident_b = held.tile([P, P], BF16, name="ident_b")
+        nc.vector.tensor_copy(ident_b[:], ident_f[:])
+
+        table_ps = flip.tile([P, S], BF16, name="table_ps")
+        for k in range(S // P):
+            nc.tensor.transpose(table_ps[:, k * P : (k + 1) * P], table_rows[:, k, :], ident_b[:])
+        table_t = held.tile([P, S], BF16, name="table_t")
+        nc.vector.tensor_copy(table_t[:], table_ps[:])
+
+        pre = [acc.tile([P, N], F32, name=f"pre{k}", tag="acc") for k in range(MB)]
+        for k in range(MB):
+            nc.tensor.matmul(
+                pre[k][:], w_emb_sb[:, k * P : (k + 1) * P], table_t[:].indirect(offsets[:]),
+                start=True, stop=False,
+            )
+
+        diff = held.tile([P, NB, 3, A], F32, name="diff")
+        nc.vector.tensor_tensor(diff[:], near[:], own[:, :, 0:3].unsqueeze(3).to_broadcast([P, NB, 3, A]), ALU.subtract)
+        nc.vector.tensor_tensor(diff[:], diff[:], diff[:], ALU.mult)
+        dist = held.tile([P, NB, A], F32, name="dist")
+        nc.vector.tensor_reduce(dist[:], diff[:].rearrange("p b a s -> p b s a"), axis=AX.X, op=ALU.add)
+        nc.vector.tensor_scalar_max(dist[:], dist[:], 1e-30)
+        nc.scalar.activation(dist[:], dist[:], ACT.Sqrt)
+
+        gsum = held.tile([P, NB, Q], F32, name="gsum")
+        for b in range(NB):
+            for q0 in range(0, Q, QC):
+                g = work.tile([P, QC, A], F32, name="g")
+                nc.vector.tensor_tensor(
+                    g[:],
+                    dist[:, b, :].unsqueeze(1).to_broadcast([P, QC, A]),
+                    centre_row[:, q0 : q0 + QC].unsqueeze(2).to_broadcast([P, QC, A]),
+                    ALU.subtract,
+                )
+                nc.scalar.activation(g[:], g[:], ACT.Square)
+                nc.scalar.activation(g[:], g[:], ACT.Exp, scale=-2.0)
+                nc.vector.tensor_reduce(gsum[:, b, q0 : q0 + QC], g[:], axis=AX.X, op=ALU.add)
+
+        rbf_ps = flip.tile([P, N], F32, name="rbf_ps")
+        for b in range(NB):
+            nc.tensor.transpose(rbf_ps[:, b * P : (b + 1) * P], gsum[:, b, :], ident_f[:])
+        rbf = held.tile([P, N], BF16, name="rbf")
+        nc.vector.tensor_scalar_mul(rbf[:], rbf_ps[:], 1.0 / A)
+
+        hid = held.tile([P, MB, N], BF16, name="hid")
+        for k in range(MB):
+            nc.tensor.matmul(pre[k][:], w_rbf_sb[:, k * P : (k + 1) * P], rbf[:], start=False, stop=True)
+            nc.scalar.activation(hid[:, k, :], pre[k][:], ACT.Gelu, bias=b1_sb[:, k : k + 1])
+        for n in range(MB):
+            out_ps = acc.tile([P, N], F32, name="out_ps", tag="acc")
+            for k in range(MB):
+                nc.tensor.matmul(
+                    out_ps[:], w2_sb[:, k, n * P : (n + 1) * P], hid[:, k, :],
+                    start=(k == 0), stop=(k == MB - 1),
+                )
+            out_sb = work.tile([P, N], F32, name="out_sb")
+            nc.vector.tensor_scalar_add(out_sb[:], out_ps[:], b2_sb[:, n : n + 1])
+            nc.sync.dma_start(out[n * P : (n + 1) * P, :], out_sb[:])

@@ -13,10 +13,13 @@ S = 512
 M = 512
 N = 256
 A = 64
+MOLS = N // A
 Q = 128
 MB = M // P
 NB = N // P
-QC = 32
+PIECES = 3
+G = 8
+PAIR = 2
 
 FLOPS = 2 * N * (P * M + Q * M + M * M)
 
@@ -25,97 +28,152 @@ def tile_frozenmlipencoder_kernel(tc, table, w_emb, coords, centers, w_rbf, b1, 
     nc = tc.nc
     with (
         tc.tile_pool(name="held", bufs=1) as held,
-        tc.tile_pool(name="work", bufs=3) as work,
-        tc.psum_pool(name="flip", bufs=1) as flip,
-        tc.psum_pool(name="acc", bufs=4) as acc,
+        tc.tile_pool(name="gauss", bufs=3) as gauss,
+        tc.tile_pool(name="store", bufs=2) as store,
+        tc.psum_pool(name="open_groups", bufs=1) as open_groups,
+        tc.psum_pool(name="bank", bufs=4) as bank,
     ):
-        offsets = held.tile([P, N // 16], U16, name="offsets")
-        nc.sync.dma_start(offsets[:], offs)
+        ident = held.tile([P, P], BF16, name="ident")
+        make_identity(nc, ident[:])
 
         near = held.tile([P, NB, 3, A], F32, name="near")
-        for mol in range(N // A):
+        for mol in range(MOLS):
             half, b = mol % 2, mol // 2
             nc.sync.dma_start(
                 near[half * A : (half + 1) * A, b, :, :],
                 coords[:, mol * A : (mol + 1) * A].unsqueeze(0).to_broadcast([A, 3, A]),
             )
+        offsets = held.tile([P, N // 16], U16, name="offsets")
+        nc.sync.dma_start(offsets[:], offs)
         own = held.tile([P, NB, 8], F32, name="own")
+        centre_col = held.tile([P, 1], F32, name="centre_col")
+        centre_row = held.tile([P, Q], F32, name="centre_row")
         b1_sb = held.tile([P, MB], F32, name="b1_sb")
         b2_sb = held.tile([P, MB], F32, name="b2_sb")
         with nc.allow_non_contiguous_dma(reason="one float to a partition: small vectors"):
             for b in range(NB):
-                nc.sync.dma_start(own[:, b, 0:3], coords[:, b * P : (b + 1) * P].rearrange("a p -> p a"))
+                nc.scalar.dma_start(own[:, b, 0:3], coords[:, b * P : (b + 1) * P].rearrange("a p -> p a"))
+            nc.scalar.dma_start(centre_row[:], centers.rearrange("q o -> o q").to_broadcast([P, Q]))
+            nc.scalar.dma_start(centre_col[:], centers)
+            table_rows = held.tile([P, S // P, P], BF16, name="table_rows")
+            nc.sync.dma_start(table_rows[:], table.rearrange("(k p) d -> p k d", p=P))
+            w_emb_sb = held.tile([P, M], BF16, name="w_emb_sb")
+            nc.scalar.dma_start(w_emb_sb[:], w_emb)
+            w_rbf_sb = held.tile([P, M], BF16, name="w_rbf_sb")
+            nc.sync.dma_start(w_rbf_sb[:], w_rbf)
+            w2_sb = held.tile([P, MB, M], BF16, name="w2_sb")
+            nc.sync.dma_start(w2_sb[:], w2.rearrange("(k p) n -> p k n", p=P))
             nc.sync.dma_start(b1_sb[:], b1.rearrange("(k p) o -> p (k o)", p=P))
             nc.sync.dma_start(b2_sb[:], b2.rearrange("(k p) o -> p (k o)", p=P))
-        centre_row = held.tile([P, Q], F32, name="centre_row")
-        nc.sync.dma_start(centre_row[:], centers.rearrange("q o -> o q").to_broadcast([P, Q]))
 
-        table_rows = held.tile([P, S // P, P], BF16, name="table_rows")
-        nc.scalar.dma_start(table_rows[:], table.rearrange("(k p) d -> p k d", p=P))
-        w_emb_sb = held.tile([P, M], BF16, name="w_emb_sb")
-        nc.scalar.dma_start(w_emb_sb[:], w_emb)
-        w_rbf_sb = held.tile([P, M], BF16, name="w_rbf_sb")
-        nc.scalar.dma_start(w_rbf_sb[:], w_rbf)
-        w2_sb = held.tile([P, MB, M], BF16, name="w2_sb")
-        nc.scalar.dma_start(w2_sb[:], w2.rearrange("(k p) n -> p k n", p=P))
+        diff = held.tile([P, NB, 3, A], F32, name="diff")
+        nc.vector.tensor_tensor(
+            diff[:], near[:], own[:, :, 0:3].unsqueeze(3).to_broadcast([P, NB, 3, A]), ALU.subtract
+        )
+        nc.vector.tensor_tensor(diff[:], diff[:], diff[:], ALU.mult)
+        dist = held.tile([P, NB, A], F32, name="dist")
+        nc.vector.tensor_tensor(dist[:], diff[:, :, 0, :], diff[:, :, 1, :], ALU.add)
+        nc.vector.scalar_tensor_tensor(dist[:], diff[:, :, 2, :], 1e-30, dist[:], ALU.max, ALU.add)
+        nc.scalar.activation(dist[:], dist[:], ACT.Sqrt)
+        dist_sq = held.tile([P, NB, A], F32, name="dist_sq")
+        nc.gpsimd.tensor_tensor(dist_sq[:], dist[:], dist[:], ALU.mult)
 
-        ident_f = held.tile([P, P], F32, name="ident_f")
-        make_identity(nc, ident_f[:])
-        ident_b = held.tile([P, P], BF16, name="ident_b")
-        nc.vector.tensor_copy(ident_b[:], ident_f[:])
+        pieces = held.tile([P, NB, 4 * 4 * A], BF16, name="pieces")
+        slots = pieces[:].rearrange("p b (i k s) -> p b i k s", i=4, k=4)
+        nc.gpsimd.memset(slots[:, :, :, PIECES, :], 0.0)
+        rest = dist[:]
+        for k in range(PIECES):
+            nc.vector.tensor_copy(slots[:, :, 0:3, k, :], rest.unsqueeze(2).to_broadcast([P, NB, 3, A]))
+            if k < PIECES - 1:
+                dist_rest = held.tile([P, NB, A], F32, name=f"dist_rest{k}")
+                nc.vector.tensor_sub(dist_rest[:], rest, slots[:, :, 0, k, :])
+                rest = dist_rest[:]
+        rest = dist_sq[:]
+        for k in range(PIECES):
+            nc.gpsimd.tensor_copy(slots[:, :, 3, k, :], rest)
+            if k < PIECES - 1:
+                sq_rest = held.tile([P, NB, A], F32, name=f"sq_rest{k}")
+                nc.gpsimd.tensor_sub(sq_rest[:], rest, slots[:, :, 3, k, :])
+                rest = sq_rest[:]
 
-        table_ps = flip.tile([P, S], BF16, name="table_ps")
+        weight_all = held.tile([P, Q], BF16, name="weight_all")
+        centre_rest = held.tile([P, Q], F32, name="centre_rest")
+        nc.vector.tensor_copy(weight_all[:], centre_row[:])
+        nc.vector.tensor_sub(centre_rest[:], centre_row[:], weight_all[:])
+        nc.vector.tensor_copy(weight_all[32:64, :], centre_rest[32:64, :])
+        nc.vector.tensor_copy(weight_all[64:96, :], centre_rest[64:96, :])
+        nc.vector.tensor_sub(centre_rest[64:96, :], centre_rest[64:96, :], weight_all[64:96, :])
+        nc.vector.tensor_copy(weight_all[64:96, :], centre_rest[64:96, :])
+        nc.vector.memset(weight_all[96:128, :], -0.5)
+        in_group = held.tile([P, G], F32, name="in_group")
+        nc.vector.tensor_reduce(in_group[:], ident[:].rearrange("p (r g) -> p g r", g=G), axis=AX.X, op=ALU.add)
+        weight = held.tile([P, G, Q], BF16, name="weight")
+        for g in range(G):
+            nc.scalar.activation(weight[:, g, :], weight_all[:], ACT.Identity, scale=in_group[:, g : g + 1])
+        exp_bias = held.tile([P, 1], F32, name="exp_bias")
+        nc.vector.scalar_tensor_tensor(exp_bias[:], centre_col[:], -2.0, centre_col[:], ALU.mult, ALU.mult)
+
+        table_ps = bank.tile([P, S], BF16, name="table_ps", tag="bank")
         for k in range(S // P):
-            nc.tensor.transpose(table_ps[:, k * P : (k + 1) * P], table_rows[:, k, :], ident_b[:])
+            nc.tensor.transpose(table_ps[:, k * P : (k + 1) * P], table_rows[:, k, :], ident[:])
         table_t = held.tile([P, S], BF16, name="table_t")
-        nc.vector.tensor_copy(table_t[:], table_ps[:])
-
-        pre = [acc.tile([P, N], F32, name=f"pre{k}", tag="acc") for k in range(MB)]
+        nc.scalar.copy(table_t[:], table_ps[:])
+        pre = [open_groups.tile([P, N], F32, name=f"pre{k}") for k in range(MB)]
         for k in range(MB):
             nc.tensor.matmul(
                 pre[k][:], w_emb_sb[:, k * P : (k + 1) * P], table_t[:].indirect(offsets[:]),
                 start=True, stop=False,
             )
 
-        diff = held.tile([P, NB, 3, A], F32, name="diff")
-        nc.vector.tensor_tensor(diff[:], near[:], own[:, :, 0:3].unsqueeze(3).to_broadcast([P, NB, 3, A]), ALU.subtract)
-        nc.vector.tensor_tensor(diff[:], diff[:], diff[:], ALU.mult)
-        dist = held.tile([P, NB, A], F32, name="dist")
-        nc.vector.tensor_reduce(dist[:], diff[:].rearrange("p b a s -> p b s a"), axis=AX.X, op=ALU.add)
-        nc.vector.tensor_scalar_max(dist[:], dist[:], 1e-30)
-        nc.scalar.activation(dist[:], dist[:], ACT.Sqrt)
+        moved = []
+        for c in range(G // PAIR):
+            moved_ps = bank.tile([P, PAIR, NB, P], BF16, name="moved_ps", tag="bank")
+            for o in range(PAIR):
+                for b in range(NB):
+                    nc.tensor.transpose(
+                        moved_ps[:, o, b, :],
+                        pieces[:, b, :].rearrange("p (c o) -> p o c", o=G)[:, c * PAIR + o, :],
+                        ident[:],
+                    )
+            moved.append(held.tile([P, PAIR, NB, P], BF16, name=f"moved{c}"))
+            nc.vector.tensor_copy(moved[c][:], moved_ps[:])
 
-        gsum = held.tile([P, NB, Q], F32, name="gsum")
-        for b in range(NB):
-            for q0 in range(0, Q, QC):
-                g = work.tile([P, QC, A], F32, name="g")
-                nc.vector.tensor_tensor(
-                    g[:],
-                    dist[:, b, :].unsqueeze(1).to_broadcast([P, QC, A]),
-                    centre_row[:, q0 : q0 + QC].unsqueeze(2).to_broadcast([P, QC, A]),
-                    ALU.subtract,
+        gauss_sum = held.tile([P, A, MOLS], F32, name="gauss_sum")
+        for c in range(G // PAIR):
+            for g in range(G):
+                arg = bank.tile([P, PAIR, MOLS, A], F32, name="arg", tag="bank")
+                nc.tensor.matmul(
+                    arg[:].rearrange("q o m t -> q (o m t)"),
+                    weight[:, g, :],
+                    moved[c][:].rearrange("r o b p -> r (o b p)"),
+                    start=True, stop=True,
                 )
-                nc.scalar.activation(g[:], g[:], ACT.Square)
-                nc.scalar.activation(g[:], g[:], ACT.Exp, scale=-2.0)
-                nc.vector.tensor_reduce(gsum[:, b, q0 : q0 + QC], g[:], axis=AX.X, op=ALU.add)
+                bell = gauss.tile([P, PAIR, MOLS, A], F32, name="bell")
+                nc.scalar.activation(bell[:], arg[:], ACT.Exp, bias=exp_bias[:, 0:1], scale=4.0)
+                s0 = G * g + PAIR * c
+                nc.vector.tensor_reduce(gauss_sum[:, s0 : s0 + PAIR, :], bell[:], axis=AX.X, op=ALU.add)
 
-        rbf_ps = flip.tile([P, N], F32, name="rbf_ps")
-        for b in range(NB):
-            nc.tensor.transpose(rbf_ps[:, b * P : (b + 1) * P], gsum[:, b, :], ident_f[:])
-        rbf = held.tile([P, N], BF16, name="rbf")
-        nc.vector.tensor_scalar_mul(rbf[:], rbf_ps[:], 1.0 / A)
+        rbf = held.tile([P, MOLS, A], BF16, name="rbf")
+        nc.vector.tensor_scalar_mul(rbf[:], gauss_sum[:].rearrange("q s m -> q m s"), 1.0 / A)
 
         hid = held.tile([P, MB, N], BF16, name="hid")
+        out_ps = [bank.tile([P, N], F32, name=f"out_ps{n}", tag="bank") for n in range(MB)]
         for k in range(MB):
-            nc.tensor.matmul(pre[k][:], w_rbf_sb[:, k * P : (k + 1) * P], rbf[:], start=False, stop=True)
+            nc.tensor.matmul(
+                pre[k][:], w_rbf_sb[:, k * P : (k + 1) * P], rbf[:].rearrange("q m s -> q (m s)"),
+                start=False, stop=True,
+            )
             nc.scalar.activation(hid[:, k, :], pre[k][:], ACT.Gelu, bias=b1_sb[:, k : k + 1])
-        for n in range(MB):
-            out_ps = acc.tile([P, N], F32, name="out_ps", tag="acc")
-            for k in range(MB):
+            for n in range(MB):
                 nc.tensor.matmul(
-                    out_ps[:], w2_sb[:, k, n * P : (n + 1) * P], hid[:, k, :],
+                    out_ps[n][:], w2_sb[:, k, n * P : (n + 1) * P], hid[:, k, :],
                     start=(k == 0), stop=(k == MB - 1),
                 )
-            out_sb = work.tile([P, N], F32, name="out_sb")
-            nc.vector.tensor_scalar_add(out_sb[:], out_ps[:], b2_sb[:, n : n + 1])
-            nc.sync.dma_start(out[n * P : (n + 1) * P, :], out_sb[:])
+        for n in range(MB):
+            out_sb = store.tile([P, N], F32, name="out_sb")
+            if n % 2 == 0:
+                nc.vector.tensor_scalar_add(out_sb[:], out_ps[n][:], b2_sb[:, n : n + 1])
+                nc.sync.dma_start(out[n * P : (n + 1) * P, :], out_sb[:])
+            else:
+                nc.scalar.activation(out_sb[:], out_ps[n][:], ACT.Identity, bias=b2_sb[:, n : n + 1])
+                nc.scalar.dma_start(out[n * P : (n + 1) * P, :], out_sb[:])

@@ -29,7 +29,7 @@ def tile_frozenmlipencoder_kernel(tc, table, w_emb, coords, centers, w_rbf, b1, 
     with (
         tc.tile_pool(name="held", bufs=1) as held,
         tc.tile_pool(name="gauss", bufs=3) as gauss,
-        tc.tile_pool(name="store", bufs=2) as store,
+        tc.tile_pool(name="store", bufs=MB) as store,
         tc.psum_pool(name="open_groups", bufs=1) as open_groups,
         tc.psum_pool(name="bank", bufs=4) as bank,
     ):
@@ -76,25 +76,21 @@ def tile_frozenmlipencoder_kernel(tc, table, w_emb, coords, centers, w_rbf, b1, 
         nc.vector.scalar_tensor_tensor(dist[:], diff[:, :, 2, :], 1e-30, dist[:], ALU.max, ALU.add)
         nc.scalar.activation(dist[:], dist[:], ACT.Sqrt)
         dist_sq = held.tile([P, NB, A], F32, name="dist_sq")
-        nc.gpsimd.tensor_tensor(dist_sq[:], dist[:], dist[:], ALU.mult)
+        nc.scalar.activation(dist_sq[:], dist[:], ACT.Square)
 
         pieces = held.tile([P, NB, 4 * 4 * A], BF16, name="pieces")
         slots = pieces[:].rearrange("p b (i k s) -> p b i k s", i=4, k=4)
         nc.gpsimd.memset(slots[:, :, :, PIECES, :], 0.0)
-        rest = dist[:]
+        dist_rest, sq_rest = dist[:], dist_sq[:]
         for k in range(PIECES):
-            nc.vector.tensor_copy(slots[:, :, 0:3, k, :], rest.unsqueeze(2).to_broadcast([P, NB, 3, A]))
+            nc.vector.tensor_copy(slots[:, :, 0:3, k, :], dist_rest.unsqueeze(2).to_broadcast([P, NB, 3, A]))
+            nc.vector.tensor_copy(slots[:, :, 3, k, :], sq_rest)
             if k < PIECES - 1:
-                dist_rest = held.tile([P, NB, A], F32, name=f"dist_rest{k}")
-                nc.vector.tensor_sub(dist_rest[:], rest, slots[:, :, 0, k, :])
-                rest = dist_rest[:]
-        rest = dist_sq[:]
-        for k in range(PIECES):
-            nc.gpsimd.tensor_copy(slots[:, :, 3, k, :], rest)
-            if k < PIECES - 1:
-                sq_rest = held.tile([P, NB, A], F32, name=f"sq_rest{k}")
-                nc.gpsimd.tensor_sub(sq_rest[:], rest, slots[:, :, 3, k, :])
-                rest = sq_rest[:]
+                dist_next = held.tile([P, NB, A], F32, name=f"dist_rest{k}")
+                nc.vector.tensor_sub(dist_next[:], dist_rest, slots[:, :, 0, k, :])
+                sq_next = held.tile([P, NB, A], F32, name=f"sq_rest{k}")
+                nc.vector.tensor_sub(sq_next[:], sq_rest, slots[:, :, 3, k, :])
+                dist_rest, sq_rest = dist_next[:], sq_next[:]
 
         weight_all = held.tile([P, Q], BF16, name="weight_all")
         centre_rest = held.tile([P, Q], F32, name="centre_rest")
@@ -109,7 +105,7 @@ def tile_frozenmlipencoder_kernel(tc, table, w_emb, coords, centers, w_rbf, b1, 
         nc.vector.tensor_reduce(in_group[:], ident[:].rearrange("p (r g) -> p g r", g=G), axis=AX.X, op=ALU.add)
         weight = held.tile([P, G, Q], BF16, name="weight")
         for g in range(G):
-            nc.scalar.activation(weight[:, g, :], weight_all[:], ACT.Identity, scale=in_group[:, g : g + 1])
+            nc.vector.tensor_scalar_mul(weight[:, g, :], weight_all[:], in_group[:, g : g + 1])
         exp_bias = held.tile([P, 1], F32, name="exp_bias")
         nc.vector.scalar_tensor_tensor(exp_bias[:], centre_col[:], -2.0, centre_col[:], ALU.mult, ALU.mult)
 

@@ -20,6 +20,7 @@ NB = N // P
 PIECES = 3
 G = 8
 PAIR = 2
+HALF = A // 2
 
 FLOPS = 2 * N * (P * M + Q * M + M * M)
 
@@ -28,7 +29,7 @@ def tile_frozenmlipencoder_kernel(tc, table, w_emb, coords, centers, w_rbf, b1, 
     nc = tc.nc
     with (
         tc.tile_pool(name="held", bufs=1) as held,
-        tc.tile_pool(name="gauss", bufs=3) as gauss,
+        tc.tile_pool(name="gauss", bufs=4) as gauss,
         tc.tile_pool(name="store", bufs=MB) as store,
         tc.psum_pool(name="open_groups", bufs=1) as open_groups,
         tc.psum_pool(name="bank", bufs=4) as bank,
@@ -121,7 +122,7 @@ def tile_frozenmlipencoder_kernel(tc, table, w_emb, coords, centers, w_rbf, b1, 
                 start=True, stop=False,
             )
 
-        moved = []
+        moved = held.tile([P, G, MOLS, A], BF16, name="moved")
         for c in range(G // PAIR):
             moved_ps = bank.tile([P, PAIR, NB, P], BF16, name="moved_ps", tag="bank")
             for o in range(PAIR):
@@ -131,26 +132,45 @@ def tile_frozenmlipencoder_kernel(tc, table, w_emb, coords, centers, w_rbf, b1, 
                         pieces[:, b, :].rearrange("p (c o) -> p o c", o=G)[:, c * PAIR + o, :],
                         ident[:],
                     )
-            moved.append(held.tile([P, PAIR, NB, P], BF16, name=f"moved{c}"))
-            nc.vector.tensor_copy(moved[c][:], moved_ps[:])
+            nc.vector.tensor_copy(
+                moved[:, c * PAIR : (c + 1) * PAIR, :, :].rearrange("r o m t -> r (o m t)"),
+                moved_ps[:].rearrange("r o b p -> r (o b p)"),
+            )
 
-        gauss_sum = held.tile([P, A, MOLS], F32, name="gauss_sum")
+        row_sum = held.tile([P, A, MOLS], F32, name="row_sum")
+        rows = row_sum[:].rearrange("q (g o) m -> q g o m", o=G)
+        mirror = held.tile([P, 2, PAIR, MOLS, HALF], F32, name="mirror")
+        nc.gpsimd.memset(mirror[:], 0.0)
+
+        def gaussians(bell, g, columns, o_first, o_count):
+            arg = bank.tile(list(bell.shape), F32, name="arg", tag="bank")
+            nc.tensor.matmul(arg[:], weight[:, g, :], columns, start=True, stop=True)
+            nc.scalar.activation(bell, arg[:], ACT.Exp, bias=exp_bias[:, 0:1], scale=4.0)
+            nc.vector.tensor_reduce(rows[:, g, o_first : o_first + o_count, :], bell, axis=AX.X, op=ALU.add)
+
         for c in range(G // PAIR):
-            for g in range(G):
-                arg = bank.tile([P, PAIR, MOLS, A], F32, name="arg", tag="bank")
-                nc.tensor.matmul(
-                    arg[:].rearrange("q o m t -> q (o m t)"),
-                    weight[:, g, :],
-                    moved[c][:].rearrange("r o b p -> r (o b p)"),
-                    start=True, stop=True,
-                )
-                bell = gauss.tile([P, PAIR, MOLS, A], F32, name="bell")
-                nc.scalar.activation(bell[:], arg[:], ACT.Exp, bias=exp_bias[:, 0:1], scale=4.0)
-                s0 = G * g + PAIR * c
-                nc.vector.tensor_reduce(gauss_sum[:, s0 : s0 + PAIR, :], bell[:], axis=AX.X, op=ALU.add)
+            for g in range(0, G // 2, 2):
+                bells = gauss.tile([P, 2, PAIR, MOLS, A], F32, name="bells")
+                for i in range(2):
+                    gaussians(bells[:, i], g + i, moved[:, c * PAIR : (c + 1) * PAIR, :, :], c * PAIR, PAIR)
+                nc.gpsimd.tensor_tensor(mirror[:], mirror[:], bells[:, :, :, :, HALF:A], ALU.add)
 
         rbf = held.tile([P, MOLS, A], BF16, name="rbf")
-        nc.vector.tensor_scalar_mul(rbf[:], gauss_sum[:].rearrange("q s m -> q m s"), 1.0 / A)
+        nc.vector.tensor_scalar_mul(rbf[:, :, 0:HALF], row_sum[:, 0:HALF, :].rearrange("q s m -> q m s"), 1.0 / A)
+
+        for c in range(G // (2 * PAIR)):
+            for g in range(G // 2, G):
+                bell = gauss.tile([P, 2 * PAIR, MOLS, HALF], F32, name="bell")
+                o_first = c * 2 * PAIR
+                gaussians(bell[:], g, moved[:, o_first : o_first + 2 * PAIR, :, HALF:A], o_first, 2 * PAIR)
+
+        nc.gpsimd.tensor_tensor(mirror[:, 0], mirror[:, 0], mirror[:, 1], ALU.add)
+        nc.gpsimd.tensor_tensor(mirror[:, 0, 0], mirror[:, 0, 0], mirror[:, 0, 1], ALU.add)
+        nc.gpsimd.tensor_scalar_mul(mirror[:, 0, 0], mirror[:, 0, 0], 1.0 / A)
+        nc.vector.scalar_tensor_tensor(
+            rbf[:, :, HALF:A], row_sum[:, HALF:A, :].rearrange("q s m -> q m s"), 1.0 / A, mirror[:, 0, 0],
+            ALU.mult, ALU.add,
+        )
 
         hid = held.tile([P, MB, N], BF16, name="hid")
         out_ps = [bank.tile([P, N], F32, name=f"out_ps{n}", tag="bank") for n in range(MB)]

@@ -29,13 +29,17 @@ def tile_frozenmlipencoder_kernel(tc, table, w_emb, coords, centers, w_rbf, b1, 
     nc = tc.nc
     with (
         tc.tile_pool(name="held", bufs=1) as held,
-        tc.tile_pool(name="gauss", bufs=4) as gauss,
+        tc.tile_pool(name="gauss", bufs=8) as gauss,
         tc.tile_pool(name="store", bufs=MB) as store,
         tc.psum_pool(name="open_groups", bufs=1) as open_groups,
         tc.psum_pool(name="bank", bufs=4) as bank,
     ):
+        ident_f = held.tile([P, P], F32, name="ident_f")
+        make_identity(nc, ident_f[:])
         ident = held.tile([P, P], BF16, name="ident")
-        make_identity(nc, ident[:])
+        nc.vector.tensor_copy(ident[:], ident_f[:])
+        in_group = held.tile([P, G], F32, name="in_group")
+        nc.vector.tensor_reduce(in_group[:], ident_f[:].rearrange("p (r g) -> p g r", g=G), axis=AX.X, op=ALU.add)
 
         near = held.tile([P, NB, 3, A], F32, name="near")
         for mol in range(MOLS):
@@ -44,71 +48,67 @@ def tile_frozenmlipencoder_kernel(tc, table, w_emb, coords, centers, w_rbf, b1, 
                 near[half * A : (half + 1) * A, b, :, :],
                 coords[:, mol * A : (mol + 1) * A].unsqueeze(0).to_broadcast([A, 3, A]),
             )
+        own_sb = held.tile([P, NB, 8], F32, name="own_sb")
+        with nc.allow_non_contiguous_dma(reason="an atom's own coordinates: three floats to a partition"):
+            for b in range(NB):
+                nc.scalar.dma_start(own_sb[:, b, 0:3], coords[:, b * P : (b + 1) * P].rearrange("a p -> p a"))
+        own = own_sb[:, :, 0:3]
+        centre_left = held.tile([P, Q], F32, name="centre_left")
+        nc.scalar.dma_start(centre_left[:], centers.rearrange("q o -> o q").to_broadcast([P, Q]))
+        vector_rows = held.tile([P, P], F32, name="vector_rows")
+        nc.vector.memset(vector_rows[:], 0.0)
+        nc.scalar.dma_start(vector_rows[0:1, :], centers.rearrange("q o -> o q"))
+        nc.scalar.dma_start(vector_rows[1 : 1 + MB, :], b1.rearrange("(k p) o -> k (p o)", p=P))
+        nc.scalar.dma_start(vector_rows[1 + MB : 1 + 2 * MB, :], b2.rearrange("(k p) o -> k (p o)", p=P))
         offsets = held.tile([P, N // 16], U16, name="offsets")
         nc.sync.dma_start(offsets[:], offs)
-        own = held.tile([P, NB, 8], F32, name="own")
-        centre_col = held.tile([P, 1], F32, name="centre_col")
-        centre_row = held.tile([P, Q], F32, name="centre_row")
-        b1_sb = held.tile([P, MB], F32, name="b1_sb")
-        b2_sb = held.tile([P, MB], F32, name="b2_sb")
-        with nc.allow_non_contiguous_dma(reason="one float to a partition: small vectors"):
-            for b in range(NB):
-                nc.scalar.dma_start(own[:, b, 0:3], coords[:, b * P : (b + 1) * P].rearrange("a p -> p a"))
-            nc.scalar.dma_start(centre_row[:], centers.rearrange("q o -> o q").to_broadcast([P, Q]))
-            nc.scalar.dma_start(centre_col[:], centers)
-            table_rows = held.tile([P, S // P, P], BF16, name="table_rows")
-            nc.sync.dma_start(table_rows[:], table.rearrange("(k p) d -> p k d", p=P))
-            w_emb_sb = held.tile([P, M], BF16, name="w_emb_sb")
-            nc.scalar.dma_start(w_emb_sb[:], w_emb)
-            w_rbf_sb = held.tile([P, M], BF16, name="w_rbf_sb")
-            nc.sync.dma_start(w_rbf_sb[:], w_rbf)
-            w2_sb = held.tile([P, MB, M], BF16, name="w2_sb")
-            nc.sync.dma_start(w2_sb[:], w2.rearrange("(k p) n -> p k n", p=P))
-            nc.sync.dma_start(b1_sb[:], b1.rearrange("(k p) o -> p (k o)", p=P))
-            nc.sync.dma_start(b2_sb[:], b2.rearrange("(k p) o -> p (k o)", p=P))
+        table_rows = held.tile([P, S // P, P], BF16, name="table_rows")
+        nc.sync.dma_start(table_rows[:], table.rearrange("(k p) d -> p k d", p=P))
+        w_emb_sb = held.tile([P, M], BF16, name="w_emb_sb")
+        nc.scalar.dma_start(w_emb_sb[:], w_emb)
+        w_rbf_sb = held.tile([P, M], BF16, name="w_rbf_sb")
+        nc.sync.dma_start(w_rbf_sb[:], w_rbf)
+        w2_sb = held.tile([P, MB, M], BF16, name="w2_sb")
+        nc.sync.dma_start(w2_sb[:], w2.rearrange("(k p) n -> p k n", p=P))
 
         diff = held.tile([P, NB, 3, A], F32, name="diff")
         nc.vector.tensor_tensor(
-            diff[:], near[:], own[:, :, 0:3].unsqueeze(3).to_broadcast([P, NB, 3, A]), ALU.subtract
+            diff[:], near[:], own.unsqueeze(3).to_broadcast([P, NB, 3, A]), ALU.subtract
         )
         nc.vector.tensor_tensor(diff[:], diff[:], diff[:], ALU.mult)
-        dist = held.tile([P, NB, A], F32, name="dist")
-        nc.vector.tensor_tensor(dist[:], diff[:, :, 0, :], diff[:, :, 1, :], ALU.add)
-        nc.vector.scalar_tensor_tensor(dist[:], diff[:, :, 2, :], 1e-30, dist[:], ALU.max, ALU.add)
-        nc.scalar.activation(dist[:], dist[:], ACT.Sqrt)
         dist_sq = held.tile([P, NB, A], F32, name="dist_sq")
-        nc.scalar.activation(dist_sq[:], dist[:], ACT.Square)
+        nc.vector.tensor_tensor(dist_sq[:], diff[:, :, 0, :], diff[:, :, 1, :], ALU.add)
+        nc.vector.scalar_tensor_tensor(dist_sq[:], diff[:, :, 2, :], 1e-30, dist_sq[:], ALU.max, ALU.add)
 
-        pieces = held.tile([P, NB, 4 * 4 * A], BF16, name="pieces")
-        slots = pieces[:].rearrange("p b (i k s) -> p b i k s", i=4, k=4)
-        nc.gpsimd.memset(slots[:, :, :, PIECES, :], 0.0)
-        dist_rest, sq_rest = dist[:], dist_sq[:]
-        for k in range(PIECES):
-            nc.vector.tensor_copy(slots[:, :, 0:3, k, :], dist_rest.unsqueeze(2).to_broadcast([P, NB, 3, A]))
-            nc.vector.tensor_copy(slots[:, :, 3, k, :], sq_rest)
-            if k < PIECES - 1:
-                dist_next = held.tile([P, NB, A], F32, name=f"dist_rest{k}")
-                nc.vector.tensor_sub(dist_next[:], dist_rest, slots[:, :, 0, k, :])
-                sq_next = held.tile([P, NB, A], F32, name=f"sq_rest{k}")
-                nc.vector.tensor_sub(sq_next[:], sq_rest, slots[:, :, 3, k, :])
-                dist_rest, sq_rest = dist_next[:], sq_next[:]
+        value = held.tile([P, NB, 4 * 4, A], F32, name="value")
+        left = value[:].rearrange("p b (i k) s -> p b i k s", k=4)
+        piece = value[:].bitcast(BF16).rearrange("p b (i k) (s h) -> p b i k s h", k=4, h=2)[:, :, :, :, :, 1]
+        nc.gpsimd.memset(left[:, :, :, PIECES, :], 0.0)
+        nc.scalar.activation(left[:, :, 0:3, 0, :], dist_sq[:].unsqueeze(2).to_broadcast([P, NB, 3, A]), ACT.Sqrt)
+        nc.scalar.activation(left[:, :, 3, 0, :], left[:, :, 0, 0, :], ACT.Square)
 
-        weight_all = held.tile([P, Q], BF16, name="weight_all")
-        centre_rest = held.tile([P, Q], F32, name="centre_rest")
-        nc.vector.tensor_copy(weight_all[:], centre_row[:])
-        nc.vector.tensor_sub(centre_rest[:], centre_row[:], weight_all[:])
-        nc.vector.tensor_copy(weight_all[32:64, :], centre_rest[32:64, :])
-        nc.vector.tensor_copy(weight_all[64:96, :], centre_rest[64:96, :])
-        nc.vector.tensor_sub(centre_rest[64:96, :], centre_rest[64:96, :], weight_all[64:96, :])
-        nc.vector.tensor_copy(weight_all[64:96, :], centre_rest[64:96, :])
-        nc.vector.memset(weight_all[96:128, :], -0.5)
-        in_group = held.tile([P, G], F32, name="in_group")
-        nc.vector.tensor_reduce(in_group[:], ident[:].rearrange("p (r g) -> p g r", g=G), axis=AX.X, op=ALU.add)
+        centre_piece = centre_left[:].bitcast(BF16).rearrange("p (q h) -> p q h", h=2)[:, :, 1]
+        nc.vector.tensor_sub(centre_left[32:64, :], centre_left[32:64, :], centre_piece[32:64, :])
+        nc.vector.tensor_sub(centre_left[64:128, :], centre_left[64:128, :], centre_piece[64:128, :])
+        nc.vector.tensor_sub(centre_left[64:96, :], centre_left[64:96, :], centre_piece[64:96, :])
+        nc.vector.memset(centre_left[96:128, :], -0.5)
+
+        for k in range(PIECES - 1):
+            nc.vector.tensor_sub(left[:, :, :, k + 1, :], left[:, :, :, k, :], piece[:, :, :, k, :])
+
         weight = held.tile([P, G, Q], BF16, name="weight")
-        for g in range(G):
-            nc.vector.tensor_scalar_mul(weight[:, g, :], weight_all[:], in_group[:, g : g + 1])
+        for g in range(G // 2):
+            nc.vector.tensor_scalar_mul(weight[:, g, :], centre_piece, in_group[:, g : g + 1])
+
+        columns_ps = bank.tile([P, P], F32, name="columns_ps", tag="bank")
+        nc.tensor.transpose(columns_ps[:], vector_rows[:], ident_f[:])
+        columns = held.tile([P, 1 + 2 * MB], F32, name="columns")
+        nc.vector.tensor_copy(columns[:], columns_ps[:, 0 : 1 + 2 * MB])
+        centre_col = columns[:, 0:1]
+        b1_sb = columns[:, 1 : 1 + MB]
+        b2_sb = columns[:, 1 + MB : 1 + 2 * MB]
         exp_bias = held.tile([P, 1], F32, name="exp_bias")
-        nc.vector.scalar_tensor_tensor(exp_bias[:], centre_col[:], -2.0, centre_col[:], ALU.mult, ALU.mult)
+        nc.vector.scalar_tensor_tensor(exp_bias[:], centre_col, -2.0, centre_col, ALU.mult, ALU.mult)
 
         table_ps = bank.tile([P, S], BF16, name="table_ps", tag="bank")
         for k in range(S // P):
@@ -122,14 +122,16 @@ def tile_frozenmlipencoder_kernel(tc, table, w_emb, coords, centers, w_rbf, b1, 
                 start=True, stop=False,
             )
 
+        halves = value[:].bitcast(BF16).rearrange("p b r x -> p b (r x)")
         moved = held.tile([P, G, MOLS, A], BF16, name="moved")
-        for c in range(G // PAIR):
+
+        def flip(c):
             moved_ps = bank.tile([P, PAIR, NB, P], BF16, name="moved_ps", tag="bank")
             for o in range(PAIR):
                 for b in range(NB):
                     nc.tensor.transpose(
                         moved_ps[:, o, b, :],
-                        pieces[:, b, :].rearrange("p (c o) -> p o c", o=G)[:, c * PAIR + o, :],
+                        halves[:, b, :].rearrange("p (c x) -> p x c", x=2 * G)[:, 2 * (c * PAIR + o) + 1, :],
                         ident[:],
                     )
             nc.vector.tensor_copy(
@@ -148,12 +150,17 @@ def tile_frozenmlipencoder_kernel(tc, table, w_emb, coords, centers, w_rbf, b1, 
             nc.scalar.activation(bell, arg[:], ACT.Exp, bias=exp_bias[:, 0:1], scale=4.0)
             nc.vector.tensor_reduce(rows[:, g, o_first : o_first + o_count, :], bell, axis=AX.X, op=ALU.add)
 
+        flip(0)
+        for g in range(G // 2, G):
+            nc.vector.tensor_scalar_mul(weight[:, g, :], centre_piece, in_group[:, g : g + 1])
         for c in range(G // PAIR):
             for g in range(0, G // 2, 2):
                 bells = gauss.tile([P, 2, PAIR, MOLS, A], F32, name="bells")
                 for i in range(2):
                     gaussians(bells[:, i], g + i, moved[:, c * PAIR : (c + 1) * PAIR, :, :], c * PAIR, PAIR)
                 nc.gpsimd.tensor_tensor(mirror[:], mirror[:], bells[:, :, :, :, HALF:A], ALU.add)
+                if g == 0 and c + 1 < G // PAIR:
+                    flip(c + 1)
 
         rbf = held.tile([P, MOLS, A], BF16, name="rbf")
         nc.vector.tensor_scalar_mul(rbf[:, :, 0:HALF], row_sum[:, 0:HALF, :].rearrange("q s m -> q m s"), 1.0 / A)

@@ -143,12 +143,12 @@ def tile_frozenmlipencoder_kernel(tc, table, w_emb, coords, centers, w_rbf, b1, 
         rows = row_sum[:].rearrange("q (g o) m -> q g o m", o=G)
         mirror = held.tile([P, 2, PAIR, MOLS, HALF], F32, name="mirror")
         nc.gpsimd.memset(mirror[:], 0.0)
+        nc.gpsimd.tensor_scalar_mul(w_rbf_sb[:], w_rbf_sb[:], 1.0 / A)
 
-        def gaussians(bell, g, columns, o_first, o_count):
+        def gaussians(bell, g, columns):
             arg = bank.tile(list(bell.shape), F32, name="arg", tag="bank")
             nc.tensor.matmul(arg[:], weight[:, g, :], columns, start=True, stop=True)
             nc.scalar.activation(bell, arg[:], ACT.Exp, bias=exp_bias[:, 0:1], scale=4.0)
-            nc.vector.tensor_reduce(rows[:, g, o_first : o_first + o_count, :], bell, axis=AX.X, op=ALU.add)
 
         flip(0)
         for g in range(G // 2, G):
@@ -157,33 +157,35 @@ def tile_frozenmlipencoder_kernel(tc, table, w_emb, coords, centers, w_rbf, b1, 
             for g in range(0, G // 2, 2):
                 bells = gauss.tile([P, 2, PAIR, MOLS, A], F32, name="bells")
                 for i in range(2):
-                    gaussians(bells[:, i], g + i, moved[:, c * PAIR : (c + 1) * PAIR, :, :], c * PAIR, PAIR)
+                    gaussians(bells[:, i], g + i, moved[:, c * PAIR : (c + 1) * PAIR, :, :])
+                nc.vector.tensor_reduce(
+                    rows[:, g : g + 2, c * PAIR : (c + 1) * PAIR, :], bells[:], axis=AX.X, op=ALU.add
+                )
                 nc.gpsimd.tensor_tensor(mirror[:], mirror[:], bells[:, :, :, :, HALF:A], ALU.add)
                 if g == 0 and c + 1 < G // PAIR:
                     flip(c + 1)
 
-        rbf = held.tile([P, MOLS, A], BF16, name="rbf")
-        nc.vector.tensor_scalar_mul(rbf[:, :, 0:HALF], row_sum[:, 0:HALF, :].rearrange("q s m -> q m s"), 1.0 / A)
+        rbf64 = held.tile([P, MOLS, A], BF16, name="rbf64")
+        nc.vector.tensor_copy(rbf64[:, :, 0:HALF], row_sum[:, 0:HALF, :].rearrange("q s m -> q m s"))
 
         for c in range(G // (2 * PAIR)):
             for g in range(G // 2, G):
                 bell = gauss.tile([P, 2 * PAIR, MOLS, HALF], F32, name="bell")
                 o_first = c * 2 * PAIR
-                gaussians(bell[:], g, moved[:, o_first : o_first + 2 * PAIR, :, HALF:A], o_first, 2 * PAIR)
+                gaussians(bell[:], g, moved[:, o_first : o_first + 2 * PAIR, :, HALF:A])
+                nc.vector.tensor_reduce(rows[:, g, o_first : o_first + 2 * PAIR, :], bell[:], axis=AX.X, op=ALU.add)
 
         nc.gpsimd.tensor_tensor(mirror[:, 0], mirror[:, 0], mirror[:, 1], ALU.add)
         nc.gpsimd.tensor_tensor(mirror[:, 0, 0], mirror[:, 0, 0], mirror[:, 0, 1], ALU.add)
-        nc.gpsimd.tensor_scalar_mul(mirror[:, 0, 0], mirror[:, 0, 0], 1.0 / A)
-        nc.vector.scalar_tensor_tensor(
-            rbf[:, :, HALF:A], row_sum[:, HALF:A, :].rearrange("q s m -> q m s"), 1.0 / A, mirror[:, 0, 0],
-            ALU.mult, ALU.add,
+        nc.vector.tensor_tensor(
+            rbf64[:, :, HALF:A], row_sum[:, HALF:A, :].rearrange("q s m -> q m s"), mirror[:, 0, 0], ALU.add
         )
 
         hid = held.tile([P, MB, N], BF16, name="hid")
         out_ps = [bank.tile([P, N], F32, name=f"out_ps{n}", tag="bank") for n in range(MB)]
         for k in range(MB):
             nc.tensor.matmul(
-                pre[k][:], w_rbf_sb[:, k * P : (k + 1) * P], rbf[:].rearrange("q m s -> q (m s)"),
+                pre[k][:], w_rbf_sb[:, k * P : (k + 1) * P], rbf64[:].rearrange("q m s -> q (m s)"),
                 start=False, stop=True,
             )
             nc.scalar.activation(hid[:, k, :], pre[k][:], ACT.Gelu, bias=b1_sb[:, k : k + 1])

@@ -145,10 +145,11 @@ def tile_frozenmlipencoder_kernel(tc, table, w_emb, coords, centers, w_rbf, b1, 
         nc.gpsimd.memset(mirror[:], 0.0)
         nc.gpsimd.tensor_scalar_mul(w_rbf_sb[:], w_rbf_sb[:], 1.0 / A)
 
-        def gaussians(bell, g, columns):
+        def gaussians(bell, g, columns, o_first, o_count):
             arg = bank.tile(list(bell.shape), F32, name="arg", tag="bank")
             nc.tensor.matmul(arg[:], weight[:, g, :], columns, start=True, stop=True)
             nc.scalar.activation(bell, arg[:], ACT.Exp, bias=exp_bias[:, 0:1], scale=4.0)
+            nc.vector.tensor_reduce(rows[:, g, o_first : o_first + o_count, :], bell, axis=AX.X, op=ALU.add)
 
         flip(0)
         for g in range(G // 2, G):
@@ -157,13 +158,10 @@ def tile_frozenmlipencoder_kernel(tc, table, w_emb, coords, centers, w_rbf, b1, 
             for g in range(0, G // 2, 2):
                 bells = gauss.tile([P, 2, PAIR, MOLS, A], F32, name="bells")
                 for i in range(2):
-                    gaussians(bells[:, i], g + i, moved[:, c * PAIR : (c + 1) * PAIR, :, :])
-                nc.vector.tensor_reduce(
-                    rows[:, g : g + 2, c * PAIR : (c + 1) * PAIR, :], bells[:], axis=AX.X, op=ALU.add
-                )
+                    gaussians(bells[:, i], g + i, moved[:, c * PAIR : (c + 1) * PAIR, :, :], c * PAIR, PAIR)
+                    if g + i == 0 and c + 1 < G // PAIR:
+                        flip(c + 1)
                 nc.gpsimd.tensor_tensor(mirror[:], mirror[:], bells[:, :, :, :, HALF:A], ALU.add)
-                if g == 0 and c + 1 < G // PAIR:
-                    flip(c + 1)
 
         rbf64 = held.tile([P, MOLS, A], BF16, name="rbf64")
         nc.vector.tensor_copy(rbf64[:, :, 0:HALF], row_sum[:, 0:HALF, :].rearrange("q s m -> q m s"))
@@ -172,8 +170,7 @@ def tile_frozenmlipencoder_kernel(tc, table, w_emb, coords, centers, w_rbf, b1, 
             for g in range(G // 2, G):
                 bell = gauss.tile([P, 2 * PAIR, MOLS, HALF], F32, name="bell")
                 o_first = c * 2 * PAIR
-                gaussians(bell[:], g, moved[:, o_first : o_first + 2 * PAIR, :, HALF:A])
-                nc.vector.tensor_reduce(rows[:, g, o_first : o_first + 2 * PAIR, :], bell[:], axis=AX.X, op=ALU.add)
+                gaussians(bell[:], g, moved[:, o_first : o_first + 2 * PAIR, :, HALF:A], o_first, 2 * PAIR)
 
         nc.gpsimd.tensor_tensor(mirror[:, 0], mirror[:, 0], mirror[:, 1], ALU.add)
         nc.gpsimd.tensor_tensor(mirror[:, 0, 0], mirror[:, 0, 0], mirror[:, 0, 1], ALU.add)

@@ -54,18 +54,18 @@ def tile_frozenmlipencoder_kernel(tc, table, w_emb, coords, centers, w_rbf, b1, 
                 nc.scalar.dma_start(own_sb[:, b, 0:3], coords[:, b * P : (b + 1) * P].rearrange("a p -> p a"))
         own = own_sb[:, :, 0:3]
         centre_left = held.tile([P, Q], F32, name="centre_left")
-        nc.scalar.dma_start(centre_left[:], centers.rearrange("q o -> o q").to_broadcast([P, Q]))
+        nc.sync.dma_start(centre_left[:], centers.rearrange("q o -> o q").to_broadcast([P, Q]))
         vector_rows = held.tile([P, P], F32, name="vector_rows")
         nc.vector.memset(vector_rows[:], 0.0)
-        nc.scalar.dma_start(vector_rows[0:1, :], centers.rearrange("q o -> o q"))
-        nc.scalar.dma_start(vector_rows[1 : 1 + MB, :], b1.rearrange("(k p) o -> k (p o)", p=P))
-        nc.scalar.dma_start(vector_rows[1 + MB : 1 + 2 * MB, :], b2.rearrange("(k p) o -> k (p o)", p=P))
+        nc.sync.dma_start(vector_rows[0:1, :], centers.rearrange("q o -> o q"))
+        nc.sync.dma_start(vector_rows[1 : 1 + MB, :], b1.rearrange("(k p) o -> k (p o)", p=P))
+        nc.sync.dma_start(vector_rows[1 + MB : 1 + 2 * MB, :], b2.rearrange("(k p) o -> k (p o)", p=P))
         offsets = held.tile([P, N // 16], U16, name="offsets")
         nc.sync.dma_start(offsets[:], offs)
         table_rows = held.tile([P, S // P, P], BF16, name="table_rows")
         nc.sync.dma_start(table_rows[:], table.rearrange("(k p) d -> p k d", p=P))
         w_emb_sb = held.tile([P, M], BF16, name="w_emb_sb")
-        nc.scalar.dma_start(w_emb_sb[:], w_emb)
+        nc.sync.dma_start(w_emb_sb[:], w_emb)
         w_rbf_sb = held.tile([P, M], BF16, name="w_rbf_sb")
         nc.sync.dma_start(w_rbf_sb[:], w_rbf)
         w2_sb = held.tile([P, MB, M], BF16, name="w2_sb")

@@ -115,12 +115,6 @@ def tile_frozenmlipencoder_kernel(tc, table, w_emb, coords, centers, w_rbf, b1, 
             nc.tensor.transpose(table_ps[:, k * P : (k + 1) * P], table_rows[:, k, :], ident[:])
         table_t = held.tile([P, S], BF16, name="table_t")
         nc.scalar.copy(table_t[:], table_ps[:])
-        pre = [open_groups.tile([P, N], F32, name=f"pre{k}") for k in range(MB)]
-        for k in range(MB):
-            nc.tensor.matmul(
-                pre[k][:], w_emb_sb[:, k * P : (k + 1) * P], table_t[:].indirect(offsets[:]),
-                start=True, stop=False,
-            )
 
         halves = value[:].bitcast(BF16).rearrange("p b r x -> p b (r x)")
         moved = held.tile([P, G, MOLS, A], BF16, name="moved")
@@ -172,6 +166,13 @@ def tile_frozenmlipencoder_kernel(tc, table, w_emb, coords, centers, w_rbf, b1, 
                 o_first = c * 2 * PAIR
                 gaussians(bell[:], g, moved[:, o_first : o_first + 2 * PAIR, :, HALF:A], o_first, 2 * PAIR)
 
+        pre = [bank.tile([P, N], F32, name=f"pre{k}", tag="bank") for k in range(MB)]
+        for k in range(MB):
+            nc.tensor.matmul(
+                pre[k][:], w_emb_sb[:, k * P : (k + 1) * P], table_t[:].indirect(offsets[:]),
+                start=True, stop=False,
+            )
+
         nc.gpsimd.tensor_tensor(mirror[:, 0], mirror[:, 0], mirror[:, 1], ALU.add)
         nc.gpsimd.tensor_tensor(mirror[:, 0, 0], mirror[:, 0, 0], mirror[:, 0, 1], ALU.add)
         nc.vector.tensor_tensor(
@@ -179,7 +180,7 @@ def tile_frozenmlipencoder_kernel(tc, table, w_emb, coords, centers, w_rbf, b1, 
         )
 
         hid = held.tile([P, MB, N], BF16, name="hid")
-        out_ps = [bank.tile([P, N], F32, name=f"out_ps{n}", tag="bank") for n in range(MB)]
+        out_ps = [open_groups.tile([P, N], F32, name=f"out_ps{n}") for n in range(MB)]
         for k in range(MB):
             nc.tensor.matmul(
                 pre[k][:], w_rbf_sb[:, k * P : (k + 1) * P], rbf64[:].rearrange("q m s -> q (m s)"),

@@ -18,8 +18,10 @@ Q = 128
 MB = M // P
 NB = N // P
 PIECES = 3
+CHUNKS = 4
 G = 8
 PAIR = 2
+SLOTS = 16
 HALF = A // 2
 
 FLOPS = 2 * N * (P * M + Q * M + M * M)
@@ -80,12 +82,18 @@ def tile_frozenmlipencoder_kernel(tc, table, w_emb, coords, centers, w_rbf, b1, 
         nc.vector.tensor_tensor(dist_sq[:], diff[:, :, 0, :], diff[:, :, 1, :], ALU.add)
         nc.vector.scalar_tensor_tensor(dist_sq[:], diff[:, :, 2, :], 1e-30, dist_sq[:], ALU.max, ALU.add)
 
-        value = held.tile([P, NB, 4 * 4, A], F32, name="value")
-        left = value[:].rearrange("p b (i k) s -> p b i k s", k=4)
-        piece = value[:].bitcast(BF16).rearrange("p b (i k) (s h) -> p b i k s h", k=4, h=2)[:, :, :, :, :, 1]
+        value = held.tile([P, NB, CHUNKS, SLOTS, G * PAIR], F32, name="value")
+        by_chunk = value[:].rearrange("p b c (i k) x -> p (b c) i k x", k=4)
+        left = value[:].rearrange("p b c (i k) x -> p b (c i) k x", k=4)
+        piece = value[:].bitcast(BF16).rearrange("p b c (i k) (x h) -> p b (c i) k x h", k=4, h=2)[:, :, :, :, :, 1]
         nc.gpsimd.memset(left[:, :, :, PIECES, :], 0.0)
-        nc.scalar.activation(left[:, :, 0:3, 0, :], dist_sq[:].unsqueeze(2).to_broadcast([P, NB, 3, A]), ACT.Sqrt)
-        nc.scalar.activation(left[:, :, 3, 0, :], left[:, :, 0, 0, :], ACT.Square)
+        nc.scalar.activation(
+            by_chunk[:, :, 0:3, 0, :],
+            dist_sq[:].rearrange("p b (c x) -> p (b c) x", c=CHUNKS).unsqueeze(2).to_broadcast(
+                [P, NB * CHUNKS, 3, G * PAIR]
+            ),
+            ACT.Sqrt,
+        )
 
         centre_piece = centre_left[:].bitcast(BF16).rearrange("p (q h) -> p q h", h=2)[:, :, 1]
         nc.vector.tensor_sub(centre_left[32:64, :], centre_left[32:64, :], centre_piece[32:64, :])
@@ -93,8 +101,14 @@ def tile_frozenmlipencoder_kernel(tc, table, w_emb, coords, centers, w_rbf, b1, 
         nc.vector.tensor_sub(centre_left[64:96, :], centre_left[64:96, :], centre_piece[64:96, :])
         nc.vector.memset(centre_left[96:128, :], -0.5)
 
-        for k in range(PIECES - 1):
-            nc.vector.tensor_sub(left[:, :, :, k + 1, :], left[:, :, :, k, :], piece[:, :, :, k, :])
+        def take_pieces(first, count):
+            whole = value[:].rearrange("p b c (i k) x -> p b c i k x", k=4)[:, :, first : first + count, :, 0, :]
+            nc.vector.tensor_tensor(whole[:, :, :, 3, :], whole[:, :, :, 0, :], whole[:, :, :, 0, :], ALU.mult)
+            these = slice(4 * first, 4 * (first + count))
+            for k in range(PIECES - 1):
+                nc.vector.tensor_sub(left[:, :, these, k + 1, :], left[:, :, these, k, :], piece[:, :, these, k, :])
+
+        take_pieces(0, 1)
 
         weight = held.tile([P, G, Q], BF16, name="weight")
         for g in range(G // 2):
@@ -114,10 +128,10 @@ def tile_frozenmlipencoder_kernel(tc, table, w_emb, coords, centers, w_rbf, b1, 
         for k in range(S // P):
             nc.tensor.transpose(table_ps[:, k * P : (k + 1) * P], table_rows[:, k, :], ident[:])
         table_t = held.tile([P, S], BF16, name="table_t")
-        nc.scalar.copy(table_t[:], table_ps[:])
+        nc.vector.tensor_copy(table_t[:], table_ps[:])
 
-        halves = value[:].bitcast(BF16).rearrange("p b r x -> p b (r x)")
-        moved = held.tile([P, G, MOLS, A], BF16, name="moved")
+        halves = value[:].bitcast(BF16).rearrange("p b c r x -> p b c (r x)")
+        moved = held.tile([P, CHUNKS, PAIR, MOLS, A], BF16, name="moved")
 
         def flip(c):
             moved_ps = bank.tile([P, PAIR, NB, P], BF16, name="moved_ps", tag="bank")
@@ -125,46 +139,50 @@ def tile_frozenmlipencoder_kernel(tc, table, w_emb, coords, centers, w_rbf, b1, 
                 for b in range(NB):
                     nc.tensor.transpose(
                         moved_ps[:, o, b, :],
-                        halves[:, b, :].rearrange("p (c x) -> p x c", x=2 * G)[:, 2 * (c * PAIR + o) + 1, :],
+                        halves[:, b, c, :].rearrange("p (n y) -> p y n", y=2 * PAIR)[:, 2 * o + 1, :],
                         ident[:],
                     )
             nc.vector.tensor_copy(
-                moved[:, c * PAIR : (c + 1) * PAIR, :, :].rearrange("r o m t -> r (o m t)"),
+                moved[:, c, :, :, :].rearrange("r o m t -> r (o m t)"),
                 moved_ps[:].rearrange("r o b p -> r (o b p)"),
             )
 
         row_sum = held.tile([P, A, MOLS], F32, name="row_sum")
-        rows = row_sum[:].rearrange("q (g o) m -> q g o m", o=G)
-        mirror = held.tile([P, 2, PAIR, MOLS, HALF], F32, name="mirror")
+        rows = row_sum[:].rearrange("q (c g o) m -> q c g (o m)", g=G, o=PAIR)
+        mirror = held.tile([P, 2, PAIR * MOLS, HALF], F32, name="mirror")
         nc.gpsimd.memset(mirror[:], 0.0)
         nc.gpsimd.tensor_scalar_mul(w_rbf_sb[:], w_rbf_sb[:], 1.0 / A)
 
-        def gaussians(bell, g, columns, o_first, o_count):
+        def gaussians(bell, g, columns, sums):
             arg = bank.tile(list(bell.shape), F32, name="arg", tag="bank")
             nc.tensor.matmul(arg[:], weight[:, g, :], columns, start=True, stop=True)
             nc.scalar.activation(bell, arg[:], ACT.Exp, bias=exp_bias[:, 0:1], scale=4.0)
-            nc.vector.tensor_reduce(rows[:, g, o_first : o_first + o_count, :], bell, axis=AX.X, op=ALU.add)
+            nc.vector.tensor_reduce(sums, bell, axis=AX.X, op=ALU.add)
 
         flip(0)
         for g in range(G // 2, G):
             nc.vector.tensor_scalar_mul(weight[:, g, :], centre_piece, in_group[:, g : g + 1])
-        for c in range(G // PAIR):
-            for g in range(0, G // 2, 2):
-                bells = gauss.tile([P, 2, PAIR, MOLS, A], F32, name="bells")
+        take_pieces(1, CHUNKS - 1)
+        for c in range(CHUNKS // 2):
+            for g in range(0, G, 2):
+                bells = gauss.tile([P, 2, PAIR * MOLS, A], F32, name="bells")
                 for i in range(2):
-                    gaussians(bells[:, i], g + i, moved[:, c * PAIR : (c + 1) * PAIR, :, :], c * PAIR, PAIR)
-                    if g + i == 0 and c + 1 < G // PAIR:
-                        flip(c + 1)
-                nc.gpsimd.tensor_tensor(mirror[:], mirror[:], bells[:, :, :, :, HALF:A], ALU.add)
+                    gaussians(
+                        bells[:, i], g + i, moved[:, c, :, :, :].rearrange("r o m t -> r (o m) t"), rows[:, c, g + i, :]
+                    )
+                if g % 4 == 0 and 2 * c + g // 4 + 1 < CHUNKS:
+                    flip(2 * c + g // 4 + 1)
+                nc.gpsimd.tensor_tensor(mirror[:], mirror[:], bells[:, :, :, HALF:A], ALU.add)
 
         rbf64 = held.tile([P, MOLS, A], BF16, name="rbf64")
         nc.vector.tensor_copy(rbf64[:, :, 0:HALF], row_sum[:, 0:HALF, :].rearrange("q s m -> q m s"))
 
-        for c in range(G // (2 * PAIR)):
-            for g in range(G // 2, G):
-                bell = gauss.tile([P, 2 * PAIR, MOLS, HALF], F32, name="bell")
-                o_first = c * 2 * PAIR
-                gaussians(bell[:], g, moved[:, o_first : o_first + 2 * PAIR, :, HALF:A], o_first, 2 * PAIR)
+        for g in range(G):
+            bell = gauss.tile([P, CHUNKS // 2, PAIR * MOLS, HALF], F32, name="bell")
+            gaussians(
+                bell[:], g, moved[:, CHUNKS // 2 :, :, :, HALF:A].rearrange("r c o m t -> r c (o m) t"),
+                rows[:, CHUNKS // 2 :, g, :],
+            )
 
         pre = [bank.tile([P, N], F32, name=f"pre{k}", tag="bank") for k in range(MB)]
         for k in range(MB):
@@ -174,9 +192,9 @@ def tile_frozenmlipencoder_kernel(tc, table, w_emb, coords, centers, w_rbf, b1, 
             )
 
         nc.gpsimd.tensor_tensor(mirror[:, 0], mirror[:, 0], mirror[:, 1], ALU.add)
-        nc.gpsimd.tensor_tensor(mirror[:, 0, 0], mirror[:, 0, 0], mirror[:, 0, 1], ALU.add)
+        nc.gpsimd.tensor_tensor(mirror[:, 0, 0:MOLS], mirror[:, 0, 0:MOLS], mirror[:, 0, MOLS : 2 * MOLS], ALU.add)
         nc.vector.tensor_tensor(
-            rbf64[:, :, HALF:A], row_sum[:, HALF:A, :].rearrange("q s m -> q m s"), mirror[:, 0, 0], ALU.add
+            rbf64[:, :, HALF:A], row_sum[:, HALF:A, :].rearrange("q s m -> q m s"), mirror[:, 0, 0:MOLS], ALU.add
         )
 
         hid = held.tile([P, MB, N], BF16, name="hid")

@@ -56,7 +56,13 @@ def tile_frozenmlipencoder_kernel(tc, table, w_emb, coords, centers, w_rbf, b1, 
                 nc.scalar.dma_start(own_sb[:, b, 0:3], coords[:, b * P : (b + 1) * P].rearrange("a p -> p a"))
         own = own_sb[:, :, 0:3]
         centre_left = held.tile([P, Q], F32, name="centre_left")
-        nc.sync.dma_start(centre_left[:], centers.rearrange("q o -> o q").to_broadcast([P, Q]))
+        nc.vector.memset(centre_left[96:128, :], -0.5)
+        nc.sync.dma_start(centre_left[0:64, :], centers.rearrange("q o -> o q").to_broadcast([64, Q]))
+        nc.sync.dma_start(centre_left[64:96, :], centers.rearrange("q o -> o q").to_broadcast([32, Q]))
+        take_off = held.tile([P, PIECES - 1], F32, name="take_off")
+        nc.vector.memset(take_off[:], 0.0)
+        nc.vector.memset(take_off[32:64, 0:1], -1.0)
+        nc.vector.memset(take_off[64:96, :], -1.0)
         vector_rows = held.tile([P, P], F32, name="vector_rows")
         nc.vector.memset(vector_rows[:], 0.0)
         nc.sync.dma_start(vector_rows[0:1, :], centers.rearrange("q o -> o q"))
@@ -96,10 +102,12 @@ def tile_frozenmlipencoder_kernel(tc, table, w_emb, coords, centers, w_rbf, b1, 
         )
 
         centre_piece = centre_left[:].bitcast(BF16).rearrange("p (q h) -> p q h", h=2)[:, :, 1]
-        nc.vector.tensor_sub(centre_left[32:64, :], centre_left[32:64, :], centre_piece[32:64, :])
-        nc.vector.tensor_sub(centre_left[64:128, :], centre_left[64:128, :], centre_piece[64:128, :])
-        nc.vector.tensor_sub(centre_left[64:96, :], centre_left[64:96, :], centre_piece[64:96, :])
-        nc.vector.memset(centre_left[96:128, :], -0.5)
+        for j in range(PIECES - 1):
+            nc.vector.scalar_tensor_tensor(
+                centre_left[:], centre_piece, take_off[:, j : j + 1], centre_left[:], ALU.mult, ALU.add
+            )
+        weight = held.tile([P, G, Q], BF16, name="weight")
+        nc.vector.tensor_scalar_mul(weight[:, 0, :], centre_piece, in_group[:, 0:1])
 
         def take_pieces(first, count):
             whole = value[:].rearrange("p b c (i k) x -> p b c i k x", k=4)[:, :, first : first + count, :, 0, :]
@@ -109,10 +117,6 @@ def tile_frozenmlipencoder_kernel(tc, table, w_emb, coords, centers, w_rbf, b1, 
                 nc.vector.tensor_sub(left[:, :, these, k + 1, :], left[:, :, these, k, :], piece[:, :, these, k, :])
 
         take_pieces(0, 1)
-
-        weight = held.tile([P, G, Q], BF16, name="weight")
-        for g in range(G // 2):
-            nc.vector.tensor_scalar_mul(weight[:, g, :], centre_piece, in_group[:, g : g + 1])
 
         columns_ps = bank.tile([P, P], F32, name="columns_ps", tag="bank")
         nc.tensor.transpose(columns_ps[:], vector_rows[:], ident_f[:])
@@ -124,11 +128,9 @@ def tile_frozenmlipencoder_kernel(tc, table, w_emb, coords, centers, w_rbf, b1, 
         exp_bias = held.tile([P, 1], F32, name="exp_bias")
         nc.vector.scalar_tensor_tensor(exp_bias[:], centre_col, -2.0, centre_col, ALU.mult, ALU.mult)
 
-        table_ps = bank.tile([P, S], BF16, name="table_ps", tag="bank")
+        table_ps = open_groups.tile([P, S], BF16, name="table_ps", tag=f"out_ps{MB - 1}")
         for k in range(S // P):
             nc.tensor.transpose(table_ps[:, k * P : (k + 1) * P], table_rows[:, k, :], ident[:])
-        table_t = held.tile([P, S], BF16, name="table_t")
-        nc.vector.tensor_copy(table_t[:], table_ps[:])
 
         halves = value[:].bitcast(BF16).rearrange("p b c r x -> p b c (r x)")
         moved = held.tile([P, CHUNKS, PAIR, MOLS, A], BF16, name="moved")
@@ -160,7 +162,7 @@ def tile_frozenmlipencoder_kernel(tc, table, w_emb, coords, centers, w_rbf, b1, 
             nc.vector.tensor_reduce(sums, bell, axis=AX.X, op=ALU.add)
 
         flip(0)
-        for g in range(G // 2, G):
+        for g in range(1, G):
             nc.vector.tensor_scalar_mul(weight[:, g, :], centre_piece, in_group[:, g : g + 1])
         take_pieces(1, CHUNKS - 1)
         for c in range(CHUNKS // 2):
@@ -176,6 +178,8 @@ def tile_frozenmlipencoder_kernel(tc, table, w_emb, coords, centers, w_rbf, b1, 
 
         rbf64 = held.tile([P, MOLS, A], BF16, name="rbf64")
         nc.vector.tensor_copy(rbf64[:, :, 0:HALF], row_sum[:, 0:HALF, :].rearrange("q s m -> q m s"))
+        table_t = held.tile([P, S], BF16, name="table_t")
+        nc.vector.tensor_copy(table_t[:], table_ps[:])
 
         for g in range(G):
             bell = gauss.tile([P, CHUNKS // 2, PAIR * MOLS, HALF], F32, name="bell")

@@ -54,7 +54,10 @@ def tile_frozenmlipencoder_kernel(tc, table, w_emb, coords, centers, w_rbf, b1, 
         with nc.allow_non_contiguous_dma(reason="an atom's own coordinates: three floats to a partition"):
             for b in range(NB):
                 nc.scalar.dma_start(own_sb[:, b, 0:3], coords[:, b * P : (b + 1) * P].rearrange("a p -> p a"))
-        own = own_sb[:, :, 0:3]
+        tiny = held.tile([P, 1], F32, name="tiny")
+        nc.vector.memset(tiny[:], 1e-30)
+        warm_up = held.tile([P, 1], F32, name="warm_up")
+        nc.scalar.activation(warm_up[:], tiny[:], ACT.Sqrt)
         centre_left = held.tile([P, Q], F32, name="centre_left")
         nc.vector.memset(centre_left[96:128, :], -0.5)
         nc.sync.dma_start(centre_left[0:64, :], centers.rearrange("q o -> o q").to_broadcast([64, Q]))
@@ -79,14 +82,21 @@ def tile_frozenmlipencoder_kernel(tc, table, w_emb, coords, centers, w_rbf, b1, 
         w2_sb = held.tile([P, MB, M], BF16, name="w2_sb")
         nc.sync.dma_start(w2_sb[:], w2.rearrange("(k p) n -> p k n", p=P))
 
-        diff = held.tile([P, NB, 3, A], F32, name="diff")
-        nc.vector.tensor_tensor(
-            diff[:], near[:], own.unsqueeze(3).to_broadcast([P, NB, 3, A]), ALU.subtract
-        )
-        nc.vector.tensor_tensor(diff[:], diff[:], diff[:], ALU.mult)
+        diff_sq = held.tile([P, NB, 3, A], F32, name="diff_sq")
+        for b in range(NB):
+            for a in range(3):
+                nc.scalar.activation(
+                    diff_sq[:, b, a, :], near[:, b, a, :], ACT.Square, bias=own_sb[:, b, a : a + 1], scale=-1.0
+                )
+
+        centre_piece = centre_left[:].bitcast(BF16).rearrange("p (q h) -> p q h", h=2)[:, :, 1]
+        for j in range(PIECES - 1):
+            nc.vector.scalar_tensor_tensor(
+                centre_left[:], centre_piece, take_off[:, j : j + 1], centre_left[:], ALU.mult, ALU.add
+            )
+
         dist_sq = held.tile([P, NB, A], F32, name="dist_sq")
-        nc.vector.tensor_tensor(dist_sq[:], diff[:, :, 0, :], diff[:, :, 1, :], ALU.add)
-        nc.vector.scalar_tensor_tensor(dist_sq[:], diff[:, :, 2, :], 1e-30, dist_sq[:], ALU.max, ALU.add)
+        nc.vector.tensor_reduce(dist_sq[:], diff_sq[:].rearrange("p b a s -> p b s a"), axis=AX.X, op=ALU.add)
 
         value = held.tile([P, NB, CHUNKS, SLOTS, G * PAIR], F32, name="value")
         by_chunk = value[:].rearrange("p b c (i k) x -> p (b c) i k x", k=4)
@@ -99,15 +109,12 @@ def tile_frozenmlipencoder_kernel(tc, table, w_emb, coords, centers, w_rbf, b1, 
                 [P, NB * CHUNKS, 3, G * PAIR]
             ),
             ACT.Sqrt,
+            bias=tiny[:, 0:1],
         )
 
-        centre_piece = centre_left[:].bitcast(BF16).rearrange("p (q h) -> p q h", h=2)[:, :, 1]
-        for j in range(PIECES - 1):
-            nc.vector.scalar_tensor_tensor(
-                centre_left[:], centre_piece, take_off[:, j : j + 1], centre_left[:], ALU.mult, ALU.add
-            )
         weight = held.tile([P, G, Q], BF16, name="weight")
-        nc.vector.tensor_scalar_mul(weight[:, 0, :], centre_piece, in_group[:, 0:1])
+        for g in range(G // 2):
+            nc.vector.tensor_scalar_mul(weight[:, g, :], centre_piece, in_group[:, g : g + 1])
 
         def take_pieces(first, count):
             whole = value[:].rearrange("p b c (i k) x -> p b c i k x", k=4)[:, :, first : first + count, :, 0, :]
@@ -162,7 +169,7 @@ def tile_frozenmlipencoder_kernel(tc, table, w_emb, coords, centers, w_rbf, b1, 
             nc.vector.tensor_reduce(sums, bell, axis=AX.X, op=ALU.add)
 
         flip(0)
-        for g in range(1, G):
+        for g in range(G // 2, G):
             nc.vector.tensor_scalar_mul(weight[:, g, :], centre_piece, in_group[:, g : g + 1])
         take_pieces(1, CHUNKS - 1)
         for c in range(CHUNKS // 2):

@@ -156,8 +156,8 @@ def tile_frozenmlipencoder_kernel(tc, table, w_emb, coords, centers, w_rbf, b1, 
                 moved_ps[:].rearrange("r o b p -> r (o b p)"),
             )
 
-        row_sum = held.tile([P, A, MOLS], F32, name="row_sum")
-        rows = row_sum[:].rearrange("q (c g o) m -> q c g (o m)", g=G, o=PAIR)
+        rbf64 = held.tile([P, MOLS, A], BF16, name="rbf64")
+        row_sum = held.tile([P, HALF, MOLS], F32, name="row_sum")
         mirror = held.tile([P, 2, PAIR * MOLS, HALF], F32, name="mirror")
         nc.gpsimd.memset(mirror[:], 0.0)
         nc.gpsimd.tensor_scalar_mul(w_rbf_sb[:], w_rbf_sb[:], 1.0 / A)
@@ -166,7 +166,8 @@ def tile_frozenmlipencoder_kernel(tc, table, w_emb, coords, centers, w_rbf, b1, 
             arg = bank.tile(list(bell.shape), F32, name="arg", tag="bank")
             nc.tensor.matmul(arg[:], weight[:, g, :], columns, start=True, stop=True)
             nc.scalar.activation(bell, arg[:], ACT.Exp, bias=exp_bias[:, 0:1], scale=4.0)
-            nc.vector.tensor_reduce(sums, bell, axis=AX.X, op=ALU.add)
+            with nc.allow_low_precision(reason="added in float32; only the finished sum is rounded, as the task asks"):
+                nc.vector.tensor_reduce(sums, bell, axis=AX.X, op=ALU.add)
 
         flip(0)
         for g in range(G // 2, G):
@@ -174,17 +175,19 @@ def tile_frozenmlipencoder_kernel(tc, table, w_emb, coords, centers, w_rbf, b1, 
         take_pieces(1, CHUNKS - 1)
         for c in range(CHUNKS // 2):
             for g in range(0, G, 2):
-                bells = gauss.tile([P, 2, PAIR * MOLS, A], F32, name="bells")
+                bells = gauss.tile([P, 2, PAIR, MOLS, A], F32, name="bells")
                 for i in range(2):
+                    lowest = G * PAIR * c + PAIR * (g + i)
                     gaussians(
-                        bells[:, i], g + i, moved[:, c, :, :, :].rearrange("r o m t -> r (o m) t"), rows[:, c, g + i, :]
+                        bells[:, i], g + i, moved[:, c, :, :, :],
+                        rbf64[:, :, lowest : lowest + PAIR].rearrange("q m o -> q o m"),
                     )
                 if g % 4 == 0 and 2 * c + g // 4 + 1 < CHUNKS:
                     flip(2 * c + g // 4 + 1)
-                nc.gpsimd.tensor_tensor(mirror[:], mirror[:], bells[:, :, :, HALF:A], ALU.add)
+                nc.gpsimd.tensor_tensor(
+                    mirror[:], mirror[:], bells[:].rearrange("q i o m t -> q i (o m) t")[:, :, :, HALF:A], ALU.add
+                )
 
-        rbf64 = held.tile([P, MOLS, A], BF16, name="rbf64")
-        nc.vector.tensor_copy(rbf64[:, :, 0:HALF], row_sum[:, 0:HALF, :].rearrange("q s m -> q m s"))
         table_t = held.tile([P, S], BF16, name="table_t")
         nc.vector.tensor_copy(table_t[:], table_ps[:])
 
@@ -192,7 +195,7 @@ def tile_frozenmlipencoder_kernel(tc, table, w_emb, coords, centers, w_rbf, b1, 
             bell = gauss.tile([P, CHUNKS // 2, PAIR * MOLS, HALF], F32, name="bell")
             gaussians(
                 bell[:], g, moved[:, CHUNKS // 2 :, :, :, HALF:A].rearrange("r c o m t -> r c (o m) t"),
-                rows[:, CHUNKS // 2 :, g, :],
+                row_sum[:].rearrange("q (c g o) m -> q c g (o m)", g=G, o=PAIR)[:, :, g, :],
             )
 
         pre = [bank.tile([P, N], F32, name=f"pre{k}", tag="bank") for k in range(MB)]
@@ -205,7 +208,7 @@ def tile_frozenmlipencoder_kernel(tc, table, w_emb, coords, centers, w_rbf, b1, 
         nc.gpsimd.tensor_tensor(mirror[:, 0], mirror[:, 0], mirror[:, 1], ALU.add)
         nc.gpsimd.tensor_tensor(mirror[:, 0, 0:MOLS], mirror[:, 0, 0:MOLS], mirror[:, 0, MOLS : 2 * MOLS], ALU.add)
         nc.vector.tensor_tensor(
-            rbf64[:, :, HALF:A], row_sum[:, HALF:A, :].rearrange("q s m -> q m s"), mirror[:, 0, 0:MOLS], ALU.add
+            rbf64[:, :, HALF:A], row_sum[:].rearrange("q s m -> q m s"), mirror[:, 0, 0:MOLS], ALU.add
         )
 
         hid = held.tile([P, MB, N], BF16, name="hid")

@@ -115,6 +115,8 @@ def tile_frozenmlipencoder_kernel(tc, table, w_emb, coords, centers, w_rbf, b1, 
         weight = held.tile([P, G, Q], BF16, name="weight")
         for g in range(G // 2):
             nc.vector.tensor_scalar_mul(weight[:, g, :], centre_piece, in_group[:, g : g + 1])
+        for g in range(G // 2, G):
+            nc.scalar.activation(weight[:, g, :], centre_piece, ACT.Copy, scale=in_group[:, g : g + 1])
 
         def take_pieces(first, count):
             whole = value[:].rearrange("p b c (i k) x -> p b c i k x", k=4)[:, :, first : first + count, :, 0, :]
@@ -151,9 +153,10 @@ def tile_frozenmlipencoder_kernel(tc, table, w_emb, coords, centers, w_rbf, b1, 
                         halves[:, b, c, :].rearrange("p (n y) -> p y n", y=2 * PAIR)[:, 2 * o + 1, :],
                         ident[:],
                     )
+            lowest_t = 0 if c < CHUNKS // 2 else HALF
             nc.vector.tensor_copy(
-                moved[:, c, :, :, :].rearrange("r o m t -> r (o m t)"),
-                moved_ps[:].rearrange("r o b p -> r (o b p)"),
+                moved[:, c, :, :, lowest_t:A].rearrange("r o m t -> r (o m) t"),
+                moved_ps[:].rearrange("r o b (h t) -> r (o b h) t", t=A)[:, :, lowest_t:A],
             )
 
         rbf64 = held.tile([P, MOLS, A], BF16, name="rbf64")
@@ -170,8 +173,6 @@ def tile_frozenmlipencoder_kernel(tc, table, w_emb, coords, centers, w_rbf, b1, 
                 nc.vector.tensor_reduce(sums, bell, axis=AX.X, op=ALU.add)
 
         flip(0)
-        for g in range(G // 2, G):
-            nc.vector.tensor_scalar_mul(weight[:, g, :], centre_piece, in_group[:, g : g + 1])
         take_pieces(1, CHUNKS - 1)
         for c in range(CHUNKS // 2):
             for g in range(0, G, 2):

@@ -220,16 +220,18 @@ def tile_frozenmlipencoder_kernel(tc, table, w_emb, coords, centers, w_rbf, b1, 
                 start=False, stop=True,
             )
             nc.scalar.activation(hid[:, k, :], pre[k][:], ACT.Gelu, bias=b1_sb[:, k : k + 1])
-            for n in range(MB):
-                nc.tensor.matmul(
-                    out_ps[n][:], w2_sb[:, k, n * P : (n + 1) * P], hid[:, k, :],
-                    start=(k == 0), stop=(k == MB - 1),
-                )
-        for n in range(MB):
-            out_sb = store.tile([P, N], F32, name="out_sb")
-            if n % 2 == 0:
-                nc.vector.tensor_scalar_add(out_sb[:], out_ps[n][:], b2_sb[:, n : n + 1])
-                nc.sync.dma_start(out[n * P : (n + 1) * P, :], out_sb[:])
-            else:
-                nc.scalar.activation(out_sb[:], out_ps[n][:], ACT.Identity, bias=b2_sb[:, n : n + 1])
-                nc.scalar.dma_start(out[n * P : (n + 1) * P, :], out_sb[:])
+        for blocks in ((0, 1), (2,), (3,)):
+            for k in range(MB):
+                for n in blocks:
+                    nc.tensor.matmul(
+                        out_ps[n][:], w2_sb[:, k, n * P : (n + 1) * P], hid[:, k, :],
+                        start=(k == 0), stop=(k == MB - 1),
+                    )
+            for n in blocks:
+                out_sb = store.tile([P, N], F32, name="out_sb")
+                if n % 2 == 0:
+                    nc.vector.tensor_scalar_add(out_sb[:], out_ps[n][:], b2_sb[:, n : n + 1])
+                    nc.sync.dma_start(out[n * P : (n + 1) * P, :], out_sb[:])
+                else:
+                    nc.scalar.activation(out_sb[:], out_ps[n][:], ACT.Identity, bias=b2_sb[:, n : n + 1])
+                    nc.scalar.dma_start(out[n * P : (n + 1) * P, :], out_sb[:])

@@ -95,6 +95,10 @@ def tile_frozenmlipencoder_kernel(tc, table, w_emb, coords, centers, w_rbf, b1, 
                 centre_left[:], centre_piece, take_off[:, j : j + 1], centre_left[:], ALU.mult, ALU.add
             )
 
+        weight = held.tile([P, G, Q], BF16, name="weight")
+        for g in range(G // 2, G):
+            nc.scalar.activation(weight[:, g, :], centre_piece, ACT.Copy, scale=in_group[:, g : g + 1])
+
         dist_sq = held.tile([P, NB, A], F32, name="dist_sq")
         nc.vector.tensor_reduce(dist_sq[:], diff_sq[:].rearrange("p b a s -> p b s a"), axis=AX.X, op=ALU.add)
 
@@ -112,11 +116,8 @@ def tile_frozenmlipencoder_kernel(tc, table, w_emb, coords, centers, w_rbf, b1, 
             bias=tiny[:, 0:1],
         )
 
-        weight = held.tile([P, G, Q], BF16, name="weight")
         for g in range(G // 2):
             nc.vector.tensor_scalar_mul(weight[:, g, :], centre_piece, in_group[:, g : g + 1])
-        for g in range(G // 2, G):
-            nc.scalar.activation(weight[:, g, :], centre_piece, ACT.Copy, scale=in_group[:, g : g + 1])
 
         def take_pieces(first, count):
             whole = value[:].rearrange("p b c (i k) x -> p b c i k x", k=4)[:, :, first : first + count, :, 0, :]
@@ -137,33 +138,28 @@ def tile_frozenmlipencoder_kernel(tc, table, w_emb, coords, centers, w_rbf, b1, 
         exp_bias = held.tile([P, 1], F32, name="exp_bias")
         nc.vector.scalar_tensor_tensor(exp_bias[:], centre_col, -2.0, centre_col, ALU.mult, ALU.mult)
 
-        table_ps = open_groups.tile([P, S], BF16, name="table_ps", tag=f"out_ps{MB - 1}")
-        for k in range(S // P):
-            nc.tensor.transpose(table_ps[:, k * P : (k + 1) * P], table_rows[:, k, :], ident[:])
-
         halves = value[:].bitcast(BF16).rearrange("p b c r x -> p b c (r x)")
         moved = held.tile([P, CHUNKS, PAIR, MOLS, A], BF16, name="moved")
 
-        def flip(c):
-            moved_ps = bank.tile([P, PAIR, NB, P], BF16, name="moved_ps", tag="bank")
-            for o in range(PAIR):
+        def flip(c, some_o):
+            moved_ps = bank.tile([P, len(some_o), NB, P], BF16, name="moved_ps", tag="bank")
+            for o in some_o:
                 for b in range(NB):
                     nc.tensor.transpose(
-                        moved_ps[:, o, b, :],
+                        moved_ps[:, o - some_o.start, b, :],
                         halves[:, b, c, :].rearrange("p (n y) -> p y n", y=2 * PAIR)[:, 2 * o + 1, :],
                         ident[:],
                     )
             lowest_t = 0 if c < CHUNKS // 2 else HALF
             nc.vector.tensor_copy(
-                moved[:, c, :, :, lowest_t:A].rearrange("r o m t -> r (o m) t"),
+                moved[:, c, some_o.start : some_o.stop, :, lowest_t:A].rearrange("r o m t -> r (o m) t"),
                 moved_ps[:].rearrange("r o b (h t) -> r (o b h) t", t=A)[:, :, lowest_t:A],
             )
 
         rbf64 = held.tile([P, MOLS, A], BF16, name="rbf64")
         row_sum = held.tile([P, HALF, MOLS], F32, name="row_sum")
         mirror = held.tile([P, 2, PAIR * MOLS, HALF], F32, name="mirror")
-        nc.gpsimd.memset(mirror[:], 0.0)
-        nc.gpsimd.tensor_scalar_mul(w_rbf_sb[:], w_rbf_sb[:], 1.0 / A)
+        late = []
 
         def gaussians(bell, g, columns, sums):
             arg = bank.tile(list(bell.shape), F32, name="arg", tag="bank")
@@ -172,22 +168,30 @@ def tile_frozenmlipencoder_kernel(tc, table, w_emb, coords, centers, w_rbf, b1, 
             with nc.allow_low_precision(reason="added in float32; only the finished sum is rounded, as the task asks"):
                 nc.vector.tensor_reduce(sums, bell, axis=AX.X, op=ALU.add)
 
-        flip(0)
+        for o in range(PAIR):
+            flip(0, range(o, o + 1))
+        nc.vector.tensor_scalar_mul(w_rbf_sb[:], w_rbf_sb[:], 1.0 / A)
         take_pieces(1, CHUNKS - 1)
+        table_ps = open_groups.tile([P, S], BF16, name="table_ps", tag=f"out_ps{MB - 1}")
         for c in range(CHUNKS // 2):
             for g in range(0, G, 2):
                 bells = gauss.tile([P, 2, PAIR, MOLS, A], F32, name="bells")
                 for i in range(2):
                     lowest = G * PAIR * c + PAIR * (g + i)
-                    gaussians(
-                        bells[:, i], g + i, moved[:, c, :, :, :],
-                        rbf64[:, :, lowest : lowest + PAIR].rearrange("q m o -> q o m"),
-                    )
-                if g % 4 == 0 and 2 * c + g // 4 + 1 < CHUNKS:
-                    flip(2 * c + g // 4 + 1)
-                nc.gpsimd.tensor_tensor(
-                    mirror[:], mirror[:], bells[:].rearrange("q i o m t -> q i (o m) t")[:, :, :, HALF:A], ALU.add
-                )
+                    width = 1 if c == 0 and g + i == 0 else PAIR
+                    for o in range(0, PAIR, width):
+                        gaussians(
+                            bells[:, i, o : o + width], g + i, moved[:, c, o : o + width, :, :],
+                            rbf64[:, :, lowest + o : lowest + o + width].rearrange("q m o -> q o m"),
+                        )
+                if g % 4 == 2 and 2 * c + g // 4 + 1 < CHUNKS:
+                    flip(2 * c + g // 4 + 1, range(PAIR))
+                elif g % 4 == 2:
+                    for k in range(S // P):
+                        nc.tensor.transpose(table_ps[:, k * P : (k + 1) * P], table_rows[:, k, :], ident[:])
+                late.append(bells[:].rearrange("q i o m t -> q i (o m) t")[:, :, :, HALF:A])
+                if len(late) > 1:
+                    nc.gpsimd.tensor_tensor(mirror[:], late[0] if len(late) == 2 else mirror[:], late[-1], ALU.add)
 
         table_t = held.tile([P, S], BF16, name="table_t")
         nc.vector.tensor_copy(table_t[:], table_ps[:])

@@ -43,6 +43,10 @@ def tile_frozenmlipencoder_kernel(tc, table, w_emb, coords, centers, w_rbf, b1, 
         in_group = held.tile([P, G], F32, name="in_group")
         nc.vector.tensor_reduce(in_group[:], ident_f[:].rearrange("p (r g) -> p g r", g=G), axis=AX.X, op=ALU.add)
 
+        own_sb = held.tile([P, NB, 8], F32, name="own_sb")
+        with nc.allow_non_contiguous_dma(reason="an atom's own coordinates: three floats to a partition"):
+            for b in range(NB):
+                nc.sync.dma_start(own_sb[:, b, 0:3], coords[:, b * P : (b + 1) * P].rearrange("a p -> p a"))
         near = held.tile([P, NB, 3, A], F32, name="near")
         for mol in range(MOLS):
             half, b = mol % 2, mol // 2
@@ -50,10 +54,6 @@ def tile_frozenmlipencoder_kernel(tc, table, w_emb, coords, centers, w_rbf, b1, 
                 near[half * A : (half + 1) * A, b, :, :],
                 coords[:, mol * A : (mol + 1) * A].unsqueeze(0).to_broadcast([A, 3, A]),
             )
-        own_sb = held.tile([P, NB, 8], F32, name="own_sb")
-        with nc.allow_non_contiguous_dma(reason="an atom's own coordinates: three floats to a partition"):
-            for b in range(NB):
-                nc.scalar.dma_start(own_sb[:, b, 0:3], coords[:, b * P : (b + 1) * P].rearrange("a p -> p a"))
         tiny = held.tile([P, 1], F32, name="tiny")
         nc.vector.memset(tiny[:], 1e-30)
         warm_up = held.tile([P, 1], F32, name="warm_up")

@@ -22,6 +22,7 @@ CHUNKS = 4
 G = 8
 PAIR = 2
 SLOTS = 16
+CHUNK = G * PAIR
 HALF = A // 2
 
 FLOPS = 2 * N * (P * M + Q * M + M * M)
@@ -141,6 +142,9 @@ def tile_frozenmlipencoder_kernel(tc, table, w_emb, coords, centers, w_rbf, b1, 
         halves = value[:].bitcast(BF16).rearrange("p b c r x -> p b c (r x)")
         moved = held.tile([P, CHUNKS, PAIR, MOLS, A], BF16, name="moved")
 
+        def first_t(c):
+            return min(CHUNK * c, HALF)
+
         def flip(c, some_o):
             moved_ps = bank.tile([P, len(some_o), NB, P], BF16, name="moved_ps", tag="bank")
             for o in some_o:
@@ -150,15 +154,15 @@ def tile_frozenmlipencoder_kernel(tc, table, w_emb, coords, centers, w_rbf, b1, 
                         halves[:, b, c, :].rearrange("p (n y) -> p y n", y=2 * PAIR)[:, 2 * o + 1, :],
                         ident[:],
                     )
-            lowest_t = 0 if c < CHUNKS // 2 else HALF
             nc.vector.tensor_copy(
-                moved[:, c, some_o.start : some_o.stop, :, lowest_t:A].rearrange("r o m t -> r (o m) t"),
-                moved_ps[:].rearrange("r o b (h t) -> r (o b h) t", t=A)[:, :, lowest_t:A],
+                moved[:, c, some_o.start : some_o.stop, :, first_t(c) : A].rearrange("r o m t -> r (o m) t"),
+                moved_ps[:].rearrange("r o b (h t) -> r (o b h) t", t=A)[:, :, first_t(c) : A],
             )
 
         rbf64 = held.tile([P, MOLS, A], BF16, name="rbf64")
-        row_sum = held.tile([P, HALF, MOLS], F32, name="row_sum")
-        mirror = held.tile([P, 2, PAIR * MOLS, HALF], F32, name="mirror")
+        row_sum = held.tile([P, A - CHUNK, MOLS], F32, name="row_sum")
+        rows = row_sum[:].rearrange("q (c g o) m -> q c g o m", g=G, o=PAIR)
+        mirror = held.tile([P, 2, PAIR * MOLS, A - CHUNK], F32, name="mirror")
         late = []
 
         def gaussians(bell, g, columns, sums):
@@ -175,23 +179,27 @@ def tile_frozenmlipencoder_kernel(tc, table, w_emb, coords, centers, w_rbf, b1, 
         table_ps = open_groups.tile([P, S], BF16, name="table_ps", tag=f"out_ps{MB - 1}")
         for c in range(CHUNKS // 2):
             for g in range(0, G, 2):
-                bells = gauss.tile([P, 2, PAIR, MOLS, A], F32, name="bells")
+                bells = gauss.tile([P, 2, PAIR, MOLS, A - first_t(c)], F32, name="bells")
                 for i in range(2):
-                    lowest = G * PAIR * c + PAIR * (g + i)
+                    lowest = PAIR * (g + i)
+                    whole_rows = rbf64[:, :, lowest : lowest + PAIR].rearrange("q m o -> q o m")
+                    sums = whole_rows if c == 0 else rows[:, c - 1, g + i]
                     width = 1 if c == 0 and g + i == 0 else PAIR
                     for o in range(0, PAIR, width):
                         gaussians(
-                            bells[:, i, o : o + width], g + i, moved[:, c, o : o + width, :, :],
-                            rbf64[:, :, lowest + o : lowest + o + width].rearrange("q m o -> q o m"),
+                            bells[:, i, o : o + width], g + i, moved[:, c, o : o + width, :, first_t(c) : A],
+                            sums[:, o : o + width],
                         )
                 if g % 4 == 2 and 2 * c + g // 4 + 1 < CHUNKS:
                     flip(2 * c + g // 4 + 1, range(PAIR))
                 elif g % 4 == 2:
                     for k in range(S // P):
                         nc.tensor.transpose(table_ps[:, k * P : (k + 1) * P], table_rows[:, k, :], ident[:])
-                late.append(bells[:].rearrange("q i o m t -> q i (o m) t")[:, :, :, HALF:A])
+                behind = CHUNK * (c + 1)
+                late.append(bells[:].rearrange("q i o m t -> q i (o m) t")[:, :, :, behind - first_t(c) :])
+                onto = mirror[:, :, :, behind - CHUNK :]
                 if len(late) > 1:
-                    nc.gpsimd.tensor_tensor(mirror[:], late[0] if len(late) == 2 else mirror[:], late[-1], ALU.add)
+                    nc.gpsimd.tensor_tensor(onto, late[0] if len(late) == 2 else onto, late[-1], ALU.add)
 
         table_t = held.tile([P, S], BF16, name="table_t")
         nc.vector.tensor_copy(table_t[:], table_ps[:])
@@ -200,7 +208,7 @@ def tile_frozenmlipencoder_kernel(tc, table, w_emb, coords, centers, w_rbf, b1, 
             bell = gauss.tile([P, CHUNKS // 2, PAIR * MOLS, HALF], F32, name="bell")
             gaussians(
                 bell[:], g, moved[:, CHUNKS // 2 :, :, :, HALF:A].rearrange("r c o m t -> r c (o m) t"),
-                row_sum[:].rearrange("q (c g o) m -> q c g (o m)", g=G, o=PAIR)[:, :, g, :],
+                rows[:, CHUNKS // 2 - 1 :, g].rearrange("q c o m -> q c (o m)"),
             )
 
         pre = [bank.tile([P, N], F32, name=f"pre{k}", tag="bank") for k in range(MB)]
@@ -213,7 +221,7 @@ def tile_frozenmlipencoder_kernel(tc, table, w_emb, coords, centers, w_rbf, b1, 
         nc.gpsimd.tensor_tensor(mirror[:, 0], mirror[:, 0], mirror[:, 1], ALU.add)
         nc.gpsimd.tensor_tensor(mirror[:, 0, 0:MOLS], mirror[:, 0, 0:MOLS], mirror[:, 0, MOLS : 2 * MOLS], ALU.add)
         nc.vector.tensor_tensor(
-            rbf64[:, :, HALF:A], row_sum[:].rearrange("q s m -> q m s"), mirror[:, 0, 0:MOLS], ALU.add
+            rbf64[:, :, CHUNK:A], row_sum[:].rearrange("q s m -> q m s"), mirror[:, 0, 0:MOLS], ALU.add
         )
 
         hid = held.tile([P, MB, N], BF16, name="hid")

@@ -162,8 +162,11 @@ def tile_frozenmlipencoder_kernel(tc, table, w_emb, coords, centers, w_rbf, b1, 
         rbf64 = held.tile([P, MOLS, A], BF16, name="rbf64")
         row_sum = held.tile([P, A - CHUNK, MOLS], F32, name="row_sum")
         rows = row_sum[:].rearrange("q (c g o) m -> q c g o m", g=G, o=PAIR)
-        mirror = held.tile([P, 2, PAIR * MOLS, A - CHUNK], F32, name="mirror")
+        column_sum = held.tile([P, MOLS, A - CHUNK], F32, name="column_sum")
+        mirror = held.tile([P, 2, PAIR * MOLS, HALF], F32, name="mirror")
         late = []
+        chunk_sum_ps = open_groups.tile([P, 2 * PAIR * MOLS, CHUNK], F32, name="chunk_sum_ps", tag=f"out_ps{MB - 2}")
+        waiting = []
 
         def gaussians(bell, g, columns, sums):
             arg = bank.tile(list(bell.shape), F32, name="arg", tag="bank")
@@ -195,12 +198,19 @@ def tile_frozenmlipencoder_kernel(tc, table, w_emb, coords, centers, w_rbf, b1, 
                 elif g % 4 == 2:
                     for k in range(S // P):
                         nc.tensor.transpose(table_ps[:, k * P : (k + 1) * P], table_rows[:, k, :], ident[:])
-                behind = CHUNK * (c + 1)
-                late.append(bells[:].rearrange("q i o m t -> q i (o m) t")[:, :, :, behind - first_t(c) :])
-                onto = mirror[:, :, :, behind - CHUNK :]
+                late.append(bells[:].rearrange("q i o m t -> q i (o m) t")[:, :, :, HALF - first_t(c) :])
                 if len(late) > 1:
-                    nc.gpsimd.tensor_tensor(onto, late[0] if len(late) == 2 else onto, late[-1], ALU.add)
+                    nc.gpsimd.tensor_tensor(mirror[:], late[0] if len(late) == 2 else mirror[:], late[-1], ALU.add)
+                if waiting:
+                    nc.tensor.matmul(
+                        chunk_sum_ps[:], ident_f[:], waiting.pop(0), start=(c == 0 and g == 2), stop=(c == 1),
+                    )
+                if c == 0:
+                    waiting.append(bells[:].rearrange("q i o m t -> q (i o m) t")[:, :, CHUNK : 2 * CHUNK])
 
+        nc.vector.tensor_reduce(
+            column_sum[:, :, 0:CHUNK], chunk_sum_ps[:].rearrange("q (r m) t -> q m t r", m=MOLS), axis=AX.X, op=ALU.add
+        )
         table_t = held.tile([P, S], BF16, name="table_t")
         nc.vector.tensor_copy(table_t[:], table_ps[:])
 
@@ -219,10 +229,8 @@ def tile_frozenmlipencoder_kernel(tc, table, w_emb, coords, centers, w_rbf, b1, 
             )
 
         nc.gpsimd.tensor_tensor(mirror[:, 0], mirror[:, 0], mirror[:, 1], ALU.add)
-        nc.gpsimd.tensor_tensor(mirror[:, 0, 0:MOLS], mirror[:, 0, 0:MOLS], mirror[:, 0, MOLS : 2 * MOLS], ALU.add)
-        nc.vector.tensor_tensor(
-            rbf64[:, :, CHUNK:A], row_sum[:].rearrange("q s m -> q m s"), mirror[:, 0, 0:MOLS], ALU.add
-        )
+        nc.gpsimd.tensor_tensor(column_sum[:, :, CHUNK:], mirror[:, 0, 0:MOLS], mirror[:, 0, MOLS : 2 * MOLS], ALU.add)
+        nc.vector.tensor_tensor(rbf64[:, :, CHUNK:A], row_sum[:].rearrange("q s m -> q m s"), column_sum[:], ALU.add)
 
         hid = held.tile([P, MB, N], BF16, name="hid")
         out_ps = [open_groups.tile([P, N], F32, name=f"out_ps{n}") for n in range(MB)]

@@ -145,17 +145,17 @@ def tile_frozenmlipencoder_kernel(tc, table, w_emb, coords, centers, w_rbf, b1, 
         def first_t(c):
             return min(CHUNK * c, HALF)
 
-        def flip(c, some_o):
-            moved_ps = bank.tile([P, len(some_o), NB, P], BF16, name="moved_ps", tag="bank")
-            for o in some_o:
+        def flip(c):
+            moved_ps = bank.tile([P, PAIR, NB, P], BF16, name="moved_ps", tag="bank")
+            for o in range(PAIR):
                 for b in range(NB):
                     nc.tensor.transpose(
-                        moved_ps[:, o - some_o.start, b, :],
+                        moved_ps[:, o, b, :],
                         halves[:, b, c, :].rearrange("p (n y) -> p y n", y=2 * PAIR)[:, 2 * o + 1, :],
                         ident[:],
                     )
             nc.vector.tensor_copy(
-                moved[:, c, some_o.start : some_o.stop, :, first_t(c) : A].rearrange("r o m t -> r (o m) t"),
+                moved[:, c, :, :, first_t(c) : A].rearrange("r o m t -> r (o m) t"),
                 moved_ps[:].rearrange("r o b (h t) -> r (o b h) t", t=A)[:, :, first_t(c) : A],
             )
 
@@ -175,8 +175,7 @@ def tile_frozenmlipencoder_kernel(tc, table, w_emb, coords, centers, w_rbf, b1, 
             with nc.allow_low_precision(reason="added in float32; only the finished sum is rounded, as the task asks"):
                 nc.vector.tensor_reduce(sums, bell, axis=AX.X, op=ALU.add)
 
-        for o in range(PAIR):
-            flip(0, range(o, o + 1))
+        flip(0)
         nc.vector.tensor_scalar_mul(w_rbf_sb[:], w_rbf_sb[:], 1.0 / A)
         take_pieces(1, CHUNKS - 1)
         table_ps = open_groups.tile([P, S], BF16, name="table_ps", tag=f"out_ps{MB - 1}")
@@ -186,15 +185,12 @@ def tile_frozenmlipencoder_kernel(tc, table, w_emb, coords, centers, w_rbf, b1, 
                 for i in range(2):
                     lowest = PAIR * (g + i)
                     whole_rows = rbf64[:, :, lowest : lowest + PAIR].rearrange("q m o -> q o m")
-                    sums = whole_rows if c == 0 else rows[:, c - 1, g + i]
-                    width = 1 if c == 0 and g + i == 0 else PAIR
-                    for o in range(0, PAIR, width):
-                        gaussians(
-                            bells[:, i, o : o + width], g + i, moved[:, c, o : o + width, :, first_t(c) : A],
-                            sums[:, o : o + width],
-                        )
+                    gaussians(
+                        bells[:, i], g + i, moved[:, c, :, :, first_t(c) : A],
+                        whole_rows if c == 0 else rows[:, c - 1, g + i],
+                    )
                 if g % 4 == 2 and 2 * c + g // 4 + 1 < CHUNKS:
-                    flip(2 * c + g // 4 + 1, range(PAIR))
+                    flip(2 * c + g // 4 + 1)
                 elif g % 4 == 2:
                     for k in range(S // P):
                         nc.tensor.transpose(table_ps[:, k * P : (k + 1) * P], table_rows[:, k, :], ident[:])

import concourse.mybir as mybir
from concourse.masks import make_identity

F32 = mybir.dt.float32
BF16 = mybir.dt.bfloat16
U16 = mybir.dt.uint16
ALU = mybir.AluOpType
ACT = mybir.ActivationFunctionType
AX = mybir.AxisListType

P = 128
S = 512
M = 512
N = 256
A = 64
MOLS = N // A
Q = 128
MB = M // P
NB = N // P
PIECES = 3
CHUNKS = 4
G = 8
PAIR = 2
SLOTS = 16
CHUNK = G * PAIR
HALF = A // 2

FLOPS = 2 * N * (P * M + Q * M + M * M)


def tile_frozenmlipencoder_kernel(tc, table, w_emb, coords, centers, w_rbf, b1, w2, b2, offs, out):
    nc = tc.nc
    with (
        tc.tile_pool(name="held", bufs=1) as held,
        tc.tile_pool(name="gauss", bufs=8) as gauss,
        tc.tile_pool(name="store", bufs=MB) as store,
        tc.psum_pool(name="open_groups", bufs=1) as open_groups,
        tc.psum_pool(name="bank", bufs=4) as bank,
    ):
        ident_f = held.tile([P, P], F32, name="ident_f")
        make_identity(nc, ident_f[:])
        ident = held.tile([P, P], BF16, name="ident")
        nc.vector.tensor_copy(ident[:], ident_f[:])
        in_group = held.tile([P, G], F32, name="in_group")
        nc.vector.tensor_reduce(in_group[:], ident_f[:].rearrange("p (r g) -> p g r", g=G), axis=AX.X, op=ALU.add)

        own_sb = held.tile([P, NB, 8], F32, name="own_sb")
        with nc.allow_non_contiguous_dma(reason="an atom's own coordinates: three floats to a partition"):
            for b in range(NB):
                nc.sync.dma_start(own_sb[:, b, 0:3], coords[:, b * P : (b + 1) * P].rearrange("a p -> p a"))
        near = held.tile([P, NB, 3, A], F32, name="near")
        for mol in range(MOLS):
            half, b = mol % 2, mol // 2
            nc.sync.dma_start(
                near[half * A : (half + 1) * A, b, :, :],
                coords[:, mol * A : (mol + 1) * A].unsqueeze(0).to_broadcast([A, 3, A]),
            )
        tiny = held.tile([P, 1], F32, name="tiny")
        nc.vector.memset(tiny[:], 1e-30)
        warm_up = held.tile([P, 1], F32, name="warm_up")
        nc.scalar.activation(warm_up[:], tiny[:], ACT.Sqrt)
        centre_left = held.tile([P, Q], F32, name="centre_left")
        nc.vector.memset(centre_left[96:128, :], -0.5)
        nc.sync.dma_start(centre_left[0:64, :], centers.rearrange("q o -> o q").to_broadcast([64, Q]))
        nc.sync.dma_start(centre_left[64:96, :], centers.rearrange("q o -> o q").to_broadcast([32, Q]))
        take_off = held.tile([P, PIECES - 1], F32, name="take_off")
        nc.vector.memset(take_off[:], 0.0)
        nc.vector.memset(take_off[32:64, 0:1], -1.0)
        nc.vector.memset(take_off[64:96, :], -1.0)
        vector_rows = held.tile([P, P], F32, name="vector_rows")
        nc.vector.memset(vector_rows[:], 0.0)
        nc.sync.dma_start(vector_rows[0:1, :], centers.rearrange("q o -> o q"))
        nc.sync.dma_start(vector_rows[1 : 1 + MB, :], b1.rearrange("(k p) o -> k (p o)", p=P))
        nc.sync.dma_start(vector_rows[1 + MB : 1 + 2 * MB, :], b2.rearrange("(k p) o -> k (p o)", p=P))
        offsets = held.tile([P, N // 16], U16, name="offsets")
        nc.sync.dma_start(offsets[:], offs)
        table_rows = held.tile([P, S // P, P], BF16, name="table_rows")
        nc.sync.dma_start(table_rows[:], table.rearrange("(k p) d -> p k d", p=P))
        w_emb_sb = held.tile([P, M], BF16, name="w_emb_sb")
        nc.sync.dma_start(w_emb_sb[:], w_emb)
        w_rbf_sb = held.tile([P, M], BF16, name="w_rbf_sb")
        nc.sync.dma_start(w_rbf_sb[:], w_rbf)
        w2_sb = held.tile([P, MB, M], BF16, name="w2_sb")
        nc.sync.dma_start(w2_sb[:], w2.rearrange("(k p) n -> p k n", p=P))

        diff_sq = held.tile([P, NB, 3, A], F32, name="diff_sq")
        for b in range(NB):
            for a in range(3):
                nc.scalar.activation(
                    diff_sq[:, b, a, :], near[:, b, a, :], ACT.Square, bias=own_sb[:, b, a : a + 1], scale=-1.0
                )

        centre_piece = centre_left[:].bitcast(BF16).rearrange("p (q h) -> p q h", h=2)[:, :, 1]
        for j in range(PIECES - 1):
            nc.vector.scalar_tensor_tensor(
                centre_left[:], centre_piece, take_off[:, j : j + 1], centre_left[:], ALU.mult, ALU.add
            )

        weight = held.tile([P, G, Q], BF16, name="weight")
        for g in range(G // 2, G):
            nc.scalar.activation(weight[:, g, :], centre_piece, ACT.Copy, scale=in_group[:, g : g + 1])

        dist_sq = held.tile([P, NB, A], F32, name="dist_sq")
        nc.vector.tensor_reduce(dist_sq[:], diff_sq[:].rearrange("p b a s -> p b s a"), axis=AX.X, op=ALU.add)

        value = held.tile([P, NB, CHUNKS, SLOTS, G * PAIR], F32, name="value")
        by_chunk = value[:].rearrange("p b c (i k) x -> p (b c) i k x", k=4)
        left = value[:].rearrange("p b c (i k) x -> p b (c i) k x", k=4)
        piece = value[:].bitcast(BF16).rearrange("p b c (i k) (x h) -> p b (c i) k x h", k=4, h=2)[:, :, :, :, :, 1]
        nc.gpsimd.memset(left[:, :, :, PIECES, :], 0.0)
        nc.scalar.activation(
            by_chunk[:, :, 0:3, 0, :],
            dist_sq[:].rearrange("p b (c x) -> p (b c) x", c=CHUNKS).unsqueeze(2).to_broadcast(
                [P, NB * CHUNKS, 3, G * PAIR]
            ),
            ACT.Sqrt,
            bias=tiny[:, 0:1],
        )

        for g in range(G // 2):
            nc.vector.tensor_scalar_mul(weight[:, g, :], centre_piece, in_group[:, g : g + 1])

        def take_pieces(first, count):
            whole = value[:].rearrange("p b c (i k) x -> p b c i k x", k=4)[:, :, first : first + count, :, 0, :]
            nc.vector.tensor_tensor(whole[:, :, :, 3, :], whole[:, :, :, 0, :], whole[:, :, :, 0, :], ALU.mult)
            these = slice(4 * first, 4 * (first + count))
            for k in range(PIECES - 1):
                nc.vector.tensor_sub(left[:, :, these, k + 1, :], left[:, :, these, k, :], piece[:, :, these, k, :])

        take_pieces(0, 1)

        columns_ps = bank.tile([P, P], F32, name="columns_ps", tag="bank")
        nc.tensor.transpose(columns_ps[:], vector_rows[:], ident_f[:])
        columns = held.tile([P, 1 + 2 * MB], F32, name="columns")
        nc.vector.tensor_copy(columns[:], columns_ps[:, 0 : 1 + 2 * MB])
        centre_col = columns[:, 0:1]
        b1_sb = columns[:, 1 : 1 + MB]
        b2_sb = columns[:, 1 + MB : 1 + 2 * MB]
        exp_bias = held.tile([P, 1], F32, name="exp_bias")
        nc.vector.scalar_tensor_tensor(exp_bias[:], centre_col, -2.0, centre_col, ALU.mult, ALU.mult)

        halves = value[:].bitcast(BF16).rearrange("p b c r x -> p b c (r x)")
        moved = held.tile([P, CHUNKS, PAIR, MOLS, A], BF16, name="moved")

        def first_t(c):
            return min(CHUNK * c, HALF)

        def flip(c):
            moved_ps = bank.tile([P, PAIR, NB, P], BF16, name="moved_ps", tag="bank")
            for o in range(PAIR):
                for b in range(NB):
                    nc.tensor.transpose(
                        moved_ps[:, o, b, :],
                        halves[:, b, c, :].rearrange("p (n y) -> p y n", y=2 * PAIR)[:, 2 * o + 1, :],
                        ident[:],
                    )
            nc.vector.tensor_copy(
                moved[:, c, :, :, first_t(c) : A].rearrange("r o m t -> r (o m) t"),
                moved_ps[:].rearrange("r o b (h t) -> r (o b h) t", t=A)[:, :, first_t(c) : A],
            )

        rbf64 = held.tile([P, MOLS, A], BF16, name="rbf64")
        row_sum = held.tile([P, A - CHUNK, MOLS], F32, name="row_sum")
        rows = row_sum[:].rearrange("q (c g o) m -> q c g o m", g=G, o=PAIR)
        column_sum = held.tile([P, MOLS, A - CHUNK], F32, name="column_sum")
        mirror = held.tile([P, 2, PAIR * MOLS, HALF], F32, name="mirror")
        late = []
        chunk_sum_ps = open_groups.tile([P, 2 * PAIR * MOLS, CHUNK], F32, name="chunk_sum_ps", tag=f"out_ps{MB - 2}")
        waiting = []

        def gaussians(bell, g, columns, sums):
            arg = bank.tile(list(bell.shape), F32, name="arg", tag="bank")
            nc.tensor.matmul(arg[:], weight[:, g, :], columns, start=True, stop=True)
            nc.scalar.activation(bell, arg[:], ACT.Exp, bias=exp_bias[:, 0:1], scale=4.0)
            with nc.allow_low_precision(reason="added in float32; only the finished sum is rounded, as the task asks"):
                nc.vector.tensor_reduce(sums, bell, axis=AX.X, op=ALU.add)

        flip(0)
        nc.vector.tensor_scalar_mul(w_rbf_sb[:], w_rbf_sb[:], 1.0 / A)
        take_pieces(1, CHUNKS - 1)
        table_ps = open_groups.tile([P, S], BF16, name="table_ps", tag=f"out_ps{MB - 1}")
        for c in range(CHUNKS // 2):
            for g in range(0, G, 2):
                bells = gauss.tile([P, 2, PAIR, MOLS, A - first_t(c)], F32, name="bells")
                for i in range(2):
                    lowest = PAIR * (g + i)
                    whole_rows = rbf64[:, :, lowest : lowest + PAIR].rearrange("q m o -> q o m")
                    gaussians(
                        bells[:, i], g + i, moved[:, c, :, :, first_t(c) : A],
                        whole_rows if c == 0 else rows[:, c - 1, g + i],
                    )
                if g % 4 == 2 and 2 * c + g // 4 + 1 < CHUNKS:
                    flip(2 * c + g // 4 + 1)
                elif g % 4 == 2:
                    for k in range(S // P):
                        nc.tensor.transpose(table_ps[:, k * P : (k + 1) * P], table_rows[:, k, :], ident[:])
                late.append(bells[:].rearrange("q i o m t -> q i (o m) t")[:, :, :, HALF - first_t(c) :])
                if len(late) > 1:
                    nc.gpsimd.tensor_tensor(mirror[:], late[0] if len(late) == 2 else mirror[:], late[-1], ALU.add)
                if waiting:
                    nc.tensor.matmul(
                        chunk_sum_ps[:], ident_f[:], waiting.pop(0), start=(c == 0 and g == 2), stop=(c == 1),
                    )
                if c == 0:
                    waiting.append(bells[:].rearrange("q i o m t -> q (i o m) t")[:, :, CHUNK : 2 * CHUNK])

        nc.vector.tensor_reduce(
            column_sum[:, :, 0:CHUNK], chunk_sum_ps[:].rearrange("q (r m) t -> q m t r", m=MOLS), axis=AX.X, op=ALU.add
        )
        table_t = held.tile([P, S], BF16, name="table_t")
        nc.vector.tensor_copy(table_t[:], table_ps[:])

        for g in range(G):
            bell = gauss.tile([P, CHUNKS // 2, PAIR * MOLS, HALF], F32, name="bell")
            gaussians(
                bell[:], g, moved[:, CHUNKS // 2 :, :, :, HALF:A].rearrange("r c o m t -> r c (o m) t"),
                rows[:, CHUNKS // 2 - 1 :, g].rearrange("q c o m -> q c (o m)"),
            )

        pre = [bank.tile([P, N], F32, name=f"pre{k}", tag="bank") for k in range(MB)]
        for k in range(MB):
            nc.tensor.matmul(
                pre[k][:], w_emb_sb[:, k * P : (k + 1) * P], table_t[:].indirect(offsets[:]),
                start=True, stop=False,
            )

        nc.gpsimd.tensor_tensor(mirror[:, 0], mirror[:, 0], mirror[:, 1], ALU.add)
        nc.gpsimd.tensor_tensor(column_sum[:, :, CHUNK:], mirror[:, 0, 0:MOLS], mirror[:, 0, MOLS : 2 * MOLS], ALU.add)
        nc.vector.tensor_tensor(rbf64[:, :, CHUNK:A], row_sum[:].rearrange("q s m -> q m s"), column_sum[:], ALU.add)

        hid = held.tile([P, MB, N], BF16, name="hid")
        out_ps = [open_groups.tile([P, N], F32, name=f"out_ps{n}") for n in range(MB)]
        for k in range(MB):
            nc.tensor.matmul(
                pre[k][:], w_rbf_sb[:, k * P : (k + 1) * P], rbf64[:].rearrange("q m s -> q (m s)"),
                start=False, stop=True,
            )
            nc.scalar.activation(hid[:, k, :], pre[k][:], ACT.Gelu, bias=b1_sb[:, k : k + 1])
        for blocks in ((0, 1), (2,), (3,)):
            for k in range(MB):
                for n in blocks:
                    nc.tensor.matmul(
                        out_ps[n][:], w2_sb[:, k, n * P : (n + 1) * P], hid[:, k, :],
                        start=(k == 0), stop=(k == MB - 1),
                    )
            for n in blocks:
                out_sb = store.tile([P, N], F32, name="out_sb")
                if n % 2 == 0:
                    nc.vector.tensor_scalar_add(out_sb[:], out_ps[n][:], b2_sb[:, n : n + 1])
                    nc.sync.dma_start(out[n * P : (n + 1) * P, :], out_sb[:])
                else:
                    nc.scalar.activation(out_sb[:], out_ps[n][:], ACT.Identity, bias=b2_sb[:, n : n + 1])
                    nc.scalar.dma_start(out[n * P : (n + 1) * P, :], out_sb[:])
